import numpy as np
import ml_dtypes


def mxq(x, axis, fmt="e4m3"):
    dtype, down = {"e4m3": (ml_dtypes.float8_e4m3fn, 7), "e5m2": (ml_dtypes.float8_e5m2, 14)}[fmt]
    v = np.moveaxis(np.asarray(x, np.float32).astype(ml_dtypes.bfloat16).astype(np.float64), axis, -1)
    blocks = v.reshape(v.shape[:-1] + (-1, 32))
    amax = np.abs(blocks).max(-1, keepdims=True)
    byte = np.maximum(np.where(amax > 0, np.frexp(amax)[1] - 1 + 127, 0) - down, 1)
    scale = np.exp2(byte - 127.0)
    codes = (blocks / scale).astype(np.float32).astype(dtype).astype(np.float64)
    return np.moveaxis((codes * scale).reshape(v.shape), -1, axis)


WIDE = False


def mx_kscale(k):
    if not WIDE:
        return np.ones(k)
    levels = np.array([10, -10, 5, -5, 0])
    a = np.random.permutation(np.resize(levels, k // 512 * 4)).reshape(k // 512, 4)
    idx = np.arange(k)
    return np.exp2(a[idx // 512, idx % 128 // 32])


BF16 = ml_dtypes.bfloat16


def bf(x):
    return np.asarray(x, np.float32).astype(BF16)


def f64(x):
    return np.asarray(x).astype(np.float64)


E2M1 = np.array([0.0, 0.5, 1.0, 1.5, 2.0, 3.0, 4.0, 6.0, -0.0, -0.5, -1.0, -1.5, -2.0, -3.0, -4.0, -6.0])


def pack_weight(w, fmt):
    k, n = w.shape
    w = f64(bf(w)).reshape(k // 32, 32, n)
    amax = np.abs(w).max(1)
    if fmt == "e4m3":
        byte = np.frexp(amax)[1] - 1 + 127 - 7
    else:
        mant, ex = np.frexp(amax / 6.0)
        byte = np.where(mant > 0.5, ex, ex - 1) + 127
    byte = np.clip(np.where(amax > 0, byte, 1), 1, 254)
    scaled = (w * np.exp2(127.0 - byte)[:, None, :]).reshape(k, n).astype(np.float32)
    by_word = np.ascontiguousarray(scaled.reshape(k // 512, 128, 4, n).transpose(0, 1, 3, 2))
    if fmt == "e4m3":
        words = by_word.astype(ml_dtypes.float8_e4m3fn).view(np.uint8)
    else:
        c = by_word.astype(ml_dtypes.float4_e2m1fn).view(np.uint8) & 0xF
        words = c[..., 0::2] | (c[..., 1::2] << 4)
    return np.ascontiguousarray(words), np.ascontiguousarray(byte.astype(np.uint8).reshape(k // 512, 16, n))


def unpack_weight(words, scales, fmt):
    g, p, n, _ = words.shape
    if fmt == "e4m3":
        vals = np.ascontiguousarray(words).view(ml_dtypes.float8_e4m3fn).astype(np.float64)
    else:
        nib = np.empty((g, p, n, 4), np.uint8)
        nib[..., 0::2] = words & 0xF
        nib[..., 1::2] = words >> 4
        vals = E2M1[nib]
    vals = vals * np.repeat(np.exp2(scales.astype(np.float64) - 127.0), 8, axis=1)[..., None]
    return vals.transpose(0, 1, 3, 2).reshape(g * 512, n)


B, D, V, H = 256, 16, 128, 512
K = D * V
LN_EPS = 1e-5


def erf(u):
    a = np.minimum(np.abs(u), 6.0)
    q = 2.0 * a * a
    t = a.copy()
    acc = a.copy()
    for n in range(1, 101):
        t *= q
        t /= 2 * n + 1
        acc += t
    return np.sign(u) * acc * np.exp(-a * a) * 2.0 / np.sqrt(np.pi)


def gelu(u):
    return 0.5 * u * (1.0 + erf(u / np.sqrt(2.0)))


def setup_inputs():
    s = mx_kscale(K)
    causal_vars = bf(np.random.standard_normal((B, D, V)) * s.reshape(D, V))
    adj_soft = bf(0.2 + 0.8 * np.random.random((D, D)))
    w1 = np.random.standard_normal((D, K, H)) * 1.5 / np.sqrt(K) / s[None, :, None]
    W1_words, W1_scales = pack_weight(w1.reshape(-1, H), "e4m3")
    b1 = bf(np.random.standard_normal((D, H)) * 0.3)
    w2 = np.random.standard_normal((D, H, V)) * 0.024 / np.sqrt(H)
    W2_words, W2_scales = pack_weight(w2.reshape(-1, V), "e4m3")
    b2 = bf(np.random.standard_normal((D, V)) * 0.006)
    gamma = bf(1.0 + 0.1 * np.random.standard_normal((D, V)))
    beta = bf(0.1 * np.random.standard_normal((D, V)))
    return {"causal_vars": causal_vars,
            "adj_soft": adj_soft,
            "W1_words": W1_words,
            "W1_scales": W1_scales,
            "b1": b1,
            "W2_words": W2_words,
            "W2_scales": W2_scales,
            "b2": b2,
            "gamma": gamma,
            "beta": beta}


def reference(causal_vars, adj_soft, W1_words, W1_scales, b1, W2_words, W2_scales, b2, gamma, beta):
    x = f64(adj_soft)[None, :, :, None] * f64(causal_vars)[:, None, :, :]
    x = x.reshape(B, D, K)
    xq = mxq(x, 2, "e4m3")
    h = (xq.transpose(1, 0, 2) @ unpack_weight(W1_words, W1_scales, "e4m3").reshape(D, K, H)).transpose(1, 0, 2) + f64(b1)[None]
    h = gelu(h)
    hq = mxq(h, 2, "e4m3")
    y = (hq.transpose(1, 0, 2) @ unpack_weight(W2_words, W2_scales, "e4m3").reshape(D, H, V)).transpose(1, 0, 2) + f64(b2)[None]
    mu = np.mean(y, axis=-1, keepdims=True)
    var = np.var(y, axis=-1, keepdims=True)
    y = (y - mu) * (1.0 / np.sqrt(var + LN_EPS))
    return y * f64(gamma)[None] + f64(beta)[None]

@@ -1,0 +1,328 @@
+import concourse.mybir as mybir
+from concourse.masks import make_identity
+
+F32 = mybir.dt.float32
+BF16 = mybir.dt.bfloat16
+I32 = mybir.dt.int32
+U32 = mybir.dt.uint32
+U8 = mybir.dt.uint8
+FP8X4 = mybir.dt.float8_e4m3fn_x4
+ALU = mybir.AluOpType
+ACT = mybir.ActivationFunctionType
+
+P = 128
+PACK = 4
+K_PASS = P * PACK
+B, D, V, H = 256, 16, 128, 512
+K = D * V
+PASSES = K // K_PASS
+B_TILES = B // P
+H_TILES = H // P
+QUADRANT = 32
+LIVE = 4
+LN_EPS = 1e-5
+FIRST_PLANES = 4
+
+FLOPS = 2 * B * D * (K * H + H * V)
+
+
+def tile_structuralequationmodels_e_kernel(
+    tc, causal_vars, adj_soft, W1_words, W1_scales, b1, W2_words, W2_scales, b2, gamma, beta, out
+):
+    nc = tc.nc
+
+    w1_words_dram = W1_words.rearrange("g p n t -> g p (n t)").bitcast(I32).rearrange("g p n -> p g n")
+    w1_scales_dram = W1_scales.bitcast(I32).rearrange("(i g) q n -> g q i n", g=PASSES)
+    w2_words_dram = W2_words.rearrange("i p v t -> i p (v t)").bitcast(I32).rearrange("i p v -> p i v")
+    w2_scales_dram = W2_scales.bitcast(I32).rearrange("i q v -> q i v")
+    cv_dram = causal_vars.rearrange("(c b) j v -> b c (j v)", b=P)
+    out_dram = out.rearrange("(c b) i v -> b c i v", b=P)
+
+    with tc.tile_pool(name="keep", bufs=1) as keep:
+        ident_f32 = keep.tile([P, P], F32)
+        ident_bf16 = keep.tile([P, P], BF16)
+        adj_col = keep.tile([P, D, PASSES], F32)
+        b1_col = keep.tile([P, D * H_TILES], F32)
+        minus_half = keep.tile([P, B_TILES], F32)
+        cv_mx = keep.tile([P, PASSES * B * PACK], BF16, align_bytes=64)
+        w1_words = [keep.tile([P, PASSES, H], I32, name="w1_words%d" % i, align_bytes=64) for i in range(D)]
+        w1_planes = keep.tile([P, D, H], U8, align_bytes=64)
+        w2_words = keep.tile([P, D, V], I32, align_bytes=64)
+        w2_planes = keep.tile([P, D, V], U8, align_bytes=64)
+        b2_rows = keep.tile([P, D * V], BF16)
+        gamma_rows = keep.tile([P, D * V], BF16)
+        beta_rows = keep.tile([P, D * V], BF16)
+
+        def load_w1_planes(first, count):
+            for quadrant in range(P // QUADRANT):
+                for g in range(PASSES):
+                    row = QUADRANT * quadrant + LIVE * g
+                    nc.sync.dma_start(
+                        out=w1_planes[row : row + LIVE, first : first + count, :].bitcast(I32),
+                        in_=w1_scales_dram[g, LIVE * quadrant : LIVE * (quadrant + 1), first : first + count, :],
+                    )
+
+        def load_w1_words(i):
+            nc.sync.dma_start(out=w1_words[i][:], in_=w1_words_dram[:, PASSES * i : PASSES * (i + 1), :])
+
+        with tc.tile_pool(name="setup", bufs=1) as setup, tc.psum_pool(name="setup_psum", bufs=1) as setup_psum:
+            cv_rows = setup.tile([P, B_TILES, K], BF16)
+            for c in range(B_TILES):
+                nc.sync.dma_start(out=cv_rows[:, c, :], in_=cv_dram[:, c, :])
+            adj_rows = setup.tile([P, D * D], BF16)
+            nc.scalar.dma_start(out=adj_rows[:], in_=adj_soft.rearrange("i j -> (i j)").partition_broadcast(P))
+            b1_rows = setup.tile([P, P], BF16)
+            nc.vector.memset(b1_rows[:], 0.0)
+            nc.scalar.dma_start(out=b1_rows[0 : D * H_TILES, :], in_=b1.rearrange("i (c m) -> (i c) m", m=P))
+            nc.vector.memset(w1_planes[:].bitcast(I32), 0)
+            nc.vector.memset(w2_planes[:].bitcast(I32), 0)
+            nc.vector.memset(minus_half[:], -0.5)
+
+            load_w1_planes(0, FIRST_PLANES)
+            for i in range(FIRST_PLANES):
+                load_w1_words(i)
+            for quadrant in range(P // QUADRANT):
+                nc.sync.dma_start(
+                    out=w2_planes[QUADRANT * quadrant : QUADRANT * quadrant + LIVE, :, :].bitcast(I32),
+                    in_=w2_scales_dram[LIVE * quadrant : LIVE * (quadrant + 1), :, :],
+                )
+            nc.sync.dma_start(out=w2_words[:], in_=w2_words_dram)
+            load_w1_planes(FIRST_PLANES, D - FIRST_PLANES)
+            load_w1_words(FIRST_PLANES)
+            nc.sync.dma_start(out=b2_rows[:], in_=b2.rearrange("i v -> (i v)").partition_broadcast(P))
+            nc.sync.dma_start(out=gamma_rows[:], in_=gamma.rearrange("i v -> (i v)").partition_broadcast(P))
+            nc.sync.dma_start(out=beta_rows[:], in_=beta.rearrange("i v -> (i v)").partition_broadcast(P))
+            for i in range(FIRST_PLANES + 1, D):
+                load_w1_words(i)
+
+            make_identity(nc, ident_f32[:])
+            make_identity(nc, ident_bf16[:])
+
+            adj_by_quadrant = adj_rows[:].rearrange("p (i g q) -> p i g q", g=PASSES, q=P // QUADRANT)
+            for quadrant in range(P // QUADRANT):
+                rows = slice(QUADRANT * quadrant, QUADRANT * (quadrant + 1))
+                nc.vector.tensor_copy(out=adj_col[rows, :, :], in_=adj_by_quadrant[rows, :, :, quadrant])
+
+            b1_psum = setup_psum.tile([P, P], BF16)
+            nc.tensor.transpose(b1_psum[:], b1_rows[:], ident_bf16[:])
+            nc.vector.tensor_copy(out=b1_col[:], in_=b1_psum[:, 0 : D * H_TILES])
+
+            for g in range(PASSES):
+                cv_psum = setup_psum.tile([P, 2, B_TILES, P], F32, name="cv_psum%d" % g)
+                for c in range(B_TILES):
+                    words = cv_rows[:, c, :].bitcast(F32)
+                    for u in range(2):
+                        nc.tensor.transpose(
+                            cv_psum[:, u, c, :],
+                            words[:, 2 * P * g + u : 2 * P * (g + 1) : 2],
+                            ident_f32[:],
+                        )
+                copy = nc.vector.tensor_copy if g % 2 == 0 else nc.scalar.copy
+                copy(
+                    out=cv_mx[:, B * PACK * g : B * PACK * (g + 1)].bitcast(F32).rearrange("p (b u) -> p b u", u=2),
+                    in_=cv_psum[:].rearrange("p u c b -> p (c b) u"),
+                )
+
+        with tc.tile_pool(name="work", bufs=2) as work, tc.psum_pool(name="psum", bufs=1) as psum:
+            live = {}
+
+            def scale_x(i):
+                x = work.tile([P, PASSES * B * PACK], BF16, name="x", align_bytes=64)
+                for g in range(PASSES):
+                    cols = slice(B * PACK * g, B * PACK * (g + 1))
+                    nc.vector.tensor_scalar_mul(out=x[:, cols], in0=cv_mx[:, cols], scalar1=adj_col[:, i, g : g + 1])
+                live["x", i] = x
+
+            def quantise_x(i):
+                x_codes = work.tile([P, PASSES * B], U32, name="x_codes", bufs=3, align_bytes=64)
+                x_plane = work.tile([P, PASSES * B], U8, name="x_plane", bufs=3, align_bytes=64)
+                nc.vector.quantize_mx(out=x_codes[:].bitcast(FP8X4), scales=x_plane[:], in_=live["x", i][:])
+                live["x_codes", i] = x_codes
+                live["x_plane", i] = x_plane
+
+            def layer1(i):
+                x_codes = live["x_codes", i]
+                x_plane = live["x_plane", i]
+                for half in range(2):
+                    h_psum = psum.tile([P, 2, B], F32, name="h_psum%d" % half, bufs=2)
+                    for c2 in range(2):
+                        n_cols = slice(P * (2 * half + c2), P * (2 * half + c2 + 1))
+                        for g in range(PASSES):
+                            b_cols = slice(B * g, B * (g + 1))
+                            nc.tensor.matmul_mx(
+                                out=h_psum[:, c2, :],
+                                lhsT=w1_words[i][:, g, n_cols].bitcast(FP8X4),
+                                lhsT_scale=w1_planes[LIVE * g : P, i, n_cols],
+                                rhs=x_codes[:, b_cols].bitcast(FP8X4),
+                                rhs_scale=x_plane[:, b_cols],
+                                start=(g == 0),
+                                stop=(g == PASSES - 1),
+                            )
+                    live["h_psum", i, half] = h_psum
+
+            def gelu(i):
+                h_cols = work.tile([P, H_TILES, B], BF16, name="h_cols")
+                for c in range(H_TILES):
+                    nc.scalar.activation(
+                        out=h_cols[:, c, :],
+                        in_=live["h_psum", i, c // 2][:, c % 2, :],
+                        func=ACT.Gelu,
+                        bias=b1_col[:, H_TILES * i + c : H_TILES * i + c + 1],
+                        scale=1.0,
+                    )
+                live["h_cols", i] = h_cols
+
+            def rows_of_h(i):
+                h_cols = live["h_cols", i]
+                h_rows_psum = psum.tile([P, B_TILES, H], BF16, name="h_rows_psum")
+                for c in range(H_TILES):
+                    for bt in range(B_TILES):
+                        nc.tensor.transpose(
+                            h_rows_psum[:, bt, P * c : P * (c + 1)], h_cols[:, c, P * bt : P * (bt + 1)], ident_bf16[:]
+                        )
+                live["h_rows_psum", i] = h_rows_psum
+
+            def sort_words(i):
+                h_rows = work.tile([P, B_TILES, 2, P], F32, name="h_rows")
+                nc.scalar.copy(
+                    out=h_rows[:],
+                    in_=live["h_rows_psum", i][:].bitcast(F32).rearrange("b c (p u) -> b c u p", u=2),
+                )
+                live["h_rows", i] = h_rows
+
+            def words_of_h(i):
+                h_rows = live["h_rows", i]
+                h_words_psum = psum.tile([P, 2, B_TILES, P], F32, name="h_words_psum")
+                for u in range(2):
+                    for bt in range(B_TILES):
+                        nc.tensor.transpose(h_words_psum[:, u, bt, :], h_rows[:, bt, u, :], ident_f32[:])
+                live["h_words_psum", i] = h_words_psum
+
+            def interleave(i):
+                h_mx = work.tile([P, B * PACK], BF16, name="h_mx", align_bytes=64)
+                nc.scalar.copy(
+                    out=h_mx[:].bitcast(F32).rearrange("p (b u) -> p b u", u=2),
+                    in_=live["h_words_psum", i][:].rearrange("p u c b -> p (c b) u"),
+                )
+                live["h_mx", i] = h_mx
+
+            def quantise_h(i):
+                h_codes = work.tile([P, B], U32, name="h_codes", align_bytes=64)
+                h_plane = work.tile([P, B], U8, name="h_plane", align_bytes=64)
+                nc.vector.quantize_mx(out=h_codes[:].bitcast(FP8X4), scales=h_plane[:], in_=live["h_mx", i][:])
+                live["h_codes", i] = h_codes
+                live["h_plane", i] = h_plane
+
+            def layer2(i):
+                h_codes = live["h_codes", i]
+                h_plane = live["h_plane", i]
+                y_psum = psum.tile([P, B_TILES, V], F32, name="y_psum", bufs=2)
+                for bt in range(B_TILES):
+                    b_cols = slice(P * bt, P * (bt + 1))
+                    nc.tensor.matmul_mx(
+                        out=y_psum[:, bt, :],
+                        lhsT=h_codes[:, b_cols].bitcast(FP8X4),
+                        lhsT_scale=h_plane[:, b_cols],
+                        rhs=w2_words[:, i, :].bitcast(FP8X4),
+                        rhs_scale=w2_planes[:, i, :],
+                        start=True,
+                        stop=True,
+                    )
+                live["y_psum", i] = y_psum
+
+            def norm_mean(i):
+                y_psum = live["y_psum", i]
+                y = work.tile([P, B_TILES, V], F32, name="y")
+                y_sum = work.tile([P, B_TILES], F32, name="y_sum", bufs=3)
+                minus_mean = work.tile([P, B_TILES], F32, name="minus_mean", bufs=3)
+                for bt in range(B_TILES):
+                    nc.vector.scalar_tensor_tensor(
+                        out=y[:, bt, :],
+                        in0=y_psum[:, bt, :],
+                        scalar=1.0,
+                        in1=b2_rows[:, V * i : V * (i + 1)],
+                        op0=ALU.mult,
+                        op1=ALU.add,
+                        accum_out=y_sum[:, bt : bt + 1],
+                    )
+                nc.gpsimd.tensor_scalar(
+                    out=minus_mean[:], in0=y_sum[:], scalar1=-1.0 / V, scalar2=0.0, op0=ALU.mult, op1=ALU.add
+                )
+                live["y", i] = y
+                live["minus_mean", i] = minus_mean
+
+            def norm_variance(i):
+                y = live["y", i]
+                minus_mean = live["minus_mean", i]
+                squares = work.tile([P, V], BF16, name="squares")
+                square_sum = work.tile([P, B_TILES], F32, name="square_sum", bufs=3)
+                var_eps = work.tile([P, B_TILES], F32, name="var_eps", bufs=3)
+                rstd = work.tile([P, B_TILES], F32, name="rstd", bufs=3)
+                for bt in range(B_TILES):
+                    nc.scalar.activation(
+                        out=squares[:],
+                        in_=y[:, bt, :],
+                        func=ACT.Square,
+                        bias=minus_mean[:, bt : bt + 1],
+                        scale=1.0,
+                        accum_out=square_sum[:, bt : bt + 1],
+                    )
+                nc.gpsimd.tensor_scalar(
+                    out=var_eps[:], in0=square_sum[:], scalar1=1.0 / V, scalar2=LN_EPS, op0=ALU.mult, op1=ALU.add
+                )
+                nc.gpsimd.tensor_tensor(out=rstd[:], in0=var_eps[:], in1=minus_half[:], op=ALU.pow)
+                live["rstd", i] = rstd
+
+            def norm_gain(i):
+                y = live["y", i]
+                minus_mean = live["minus_mean", i]
+                centred = work.tile([P, B_TILES, V], F32, name="centred")
+                for bt in range(B_TILES):
+                    nc.vector.scalar_tensor_tensor(
+                        out=centred[:, bt, :],
+                        in0=y[:, bt, :],
+                        scalar=minus_mean[:, bt : bt + 1],
+                        in1=gamma_rows[:, V * i : V * (i + 1)],
+                        op0=ALU.add,
+                        op1=ALU.mult,
+                    )
+                live["centred", i] = centred
+
+            def norm_shift_and_store(i):
+                centred = live["centred", i]
+                rstd = live["rstd", i]
+                result = work.tile([P, B_TILES, V], F32, name="result", bufs=3)
+                for bt in range(B_TILES):
+                    nc.vector.scalar_tensor_tensor(
+                        out=result[:, bt, :],
+                        in0=centred[:, bt, :],
+                        scalar=rstd[:, bt : bt + 1],
+                        in1=beta_rows[:, V * i : V * (i + 1)],
+                        op0=ALU.mult,
+                        op1=ALU.add,
+                    )
+                nc.sync.dma_start(out=out_dram[:, :, i, :], in_=result[:])
+
+            def run(stage, i):
+                if 0 <= i < D:
+                    stage(i)
+
+            with tc.manual_schedule():
+                for i in range(2):
+                    scale_x(i)
+                    quantise_x(i)
+                for s in range(D + 6):
+                    run(norm_shift_and_store, s - 5)
+                    run(sort_words, s - 2)
+                    run(norm_mean, s - 4)
+                    run(gelu, s - 1)
+                    run(scale_x, s + 2)
+                    run(interleave, s - 3)
+                    run(norm_gain, s - 4)
+                    run(norm_variance, s - 4)
+                    run(quantise_h, s - 3)
+                    run(quantise_x, s + 2)
+                    run(layer1, s)
+                    run(words_of_h, s - 2)
+                    run(rows_of_h, s - 1)
+                    run(layer2, s - 3)

@@ -1,3 +1,5 @@
+from contextlib import ExitStack
+
 import concourse.mybir as mybir
 from concourse.masks import make_identity
 
@@ -19,9 +21,12 @@ PASSES = K // K_PASS
 B_TILES = B // P
 H_TILES = H // P
 QUADRANT = 32
+QUADRANTS = P // QUADRANT
 LIVE = 4
+BANK = 512
 LN_EPS = 1e-5
-FIRST_PLANES = 4
+PLANE_GROUP = 4
+LOOKAHEAD = 4
 
 FLOPS = 2 * B * D * (K * H + H * V)
 
@@ -38,7 +43,15 @@ def tile_structuralequationmodels_e_kernel(
     cv_dram = causal_vars.rearrange("(c b) j v -> b c (j v)", b=P)
     out_dram = out.rearrange("(c b) i v -> b c i v", b=P)
 
-    with tc.tile_pool(name="keep", bufs=1) as keep:
+    with ExitStack() as ctx:
+        ctx.enter_context(tc.manual_schedule())
+        keep = ctx.enter_context(tc.tile_pool(name="keep", bufs=1))
+        work = ctx.enter_context(tc.tile_pool(name="work", bufs=2))
+        psum = ctx.enter_context(tc.psum_pool(name="psum", bufs=1))
+
+        def bank(k, shape, dtype, name):
+            return psum.tile(shape, dtype, name=name, tag="bank%d" % k)
+
         ident_f32 = keep.tile([P, P], F32)
         ident_bf16 = keep.tile([P, P], BF16)
         adj_col = keep.tile([P, D, PASSES], F32)
@@ -52,277 +65,278 @@ def tile_structuralequationmodels_e_kernel(
         b2_rows = keep.tile([P, D * V], BF16)
         gamma_rows = keep.tile([P, D * V], BF16)
         beta_rows = keep.tile([P, D * V], BF16)
+        cv_rows = keep.tile([P, B_TILES, K], BF16)
+        vectors = keep.tile([P, D * V], BF16)
+        select = keep.tile([P, QUADRANTS, P], BF16)
+        b1_rows = keep.tile([P, P], BF16)
 
-        def load_w1_planes(first, count):
-            for quadrant in range(P // QUADRANT):
-                for g in range(PASSES):
-                    row = QUADRANT * quadrant + LIVE * g
-                    nc.sync.dma_start(
-                        out=w1_planes[row : row + LIVE, first : first + count, :].bitcast(I32),
-                        in_=w1_scales_dram[g, LIVE * quadrant : LIVE * (quadrant + 1), first : first + count, :],
-                    )
-
-        def load_w1_words(i):
+        def load_equation(i):
+            if i % PLANE_GROUP == 0:
+                group = slice(i, i + PLANE_GROUP)
+                for quadrant in range(QUADRANTS):
+                    for r in range(LIVE):
+                        first = QUADRANT * quadrant + r
+                        nc.sync.dma_start(
+                            out=w1_planes[first : first + LIVE * PASSES : LIVE, group, :].bitcast(I32),
+                            in_=w1_scales_dram[:, LIVE * quadrant + r, group, :],
+                        )
             nc.sync.dma_start(out=w1_words[i][:], in_=w1_words_dram[:, PASSES * i : PASSES * (i + 1), :])
 
-        with tc.tile_pool(name="setup", bufs=1) as setup, tc.psum_pool(name="setup_psum", bufs=1) as setup_psum:
-            cv_rows = setup.tile([P, B_TILES, K], BF16)
+        for c in range(B_TILES):
+            nc.sync.dma_start(out=cv_rows[:, c, :], in_=cv_dram[:, c, :])
+        nc.vector.memset(vectors[:], 0.0)
+        nc.vector.memset(b1_rows[:], 0.0)
+        nc.vector.memset(select[:], 0.0)
+        for r in range(QUADRANTS):
+            nc.vector.memset(select[QUADRANT * r : QUADRANT * r + 1, r, :], 1.0)
+        for r, vector in enumerate((b2, gamma, beta, adj_soft)):
+            row = vector.rearrange("i v -> (i v)").unsqueeze(0)
+            nc.scalar.dma_start(out=vectors[QUADRANT * r : QUADRANT * r + 1, 0 : row.shape[1]], in_=row)
+        nc.scalar.dma_start(out=b1_rows[0 : D * H_TILES, :], in_=b1.rearrange("i (c m) -> (i c) m", m=P))
+        nc.vector.memset(w1_planes[:].bitcast(I32), 0)
+        nc.vector.memset(w2_planes[:].bitcast(I32), 0)
+        for i in range(LOOKAHEAD):
+            load_equation(i)
+        for quadrant in range(QUADRANTS):
+            nc.sync.dma_start(
+                out=w2_planes[QUADRANT * quadrant : QUADRANT * quadrant + LIVE, :, :].bitcast(I32),
+                in_=w2_scales_dram[LIVE * quadrant : LIVE * (quadrant + 1), :, :],
+            )
+        nc.sync.dma_start(out=w2_words[:], in_=w2_words_dram)
+
+        nc.vector.memset(minus_half[:], -0.5)
+        make_identity(nc, ident_f32[:])
+        make_identity(nc, ident_bf16[:])
+
+        adj_psum = bank(4, [P, D * D], F32, "adj_psum")
+        nc.tensor.matmul(adj_psum[:], lhsT=select[:, 3, :], rhs=vectors[:, 0 : D * D], start=True, stop=True)
+        adj_by_quadrant = adj_psum[:].rearrange("p (i g q) -> p i g q", g=PASSES, q=QUADRANTS)
+        for quadrant in range(QUADRANTS):
+            rows = slice(QUADRANT * quadrant, QUADRANT * (quadrant + 1))
+            nc.vector.tensor_copy(out=adj_col[rows, :, :], in_=adj_by_quadrant[rows, :, :, quadrant])
+
+        b1_psum = bank(5, [P, P], BF16, "b1_psum")
+        nc.tensor.transpose(b1_psum[:], b1_rows[:], ident_bf16[:])
+        nc.vector.tensor_copy(out=b1_col[:], in_=b1_psum[:, 0 : D * H_TILES])
+
+        for g in range(PASSES):
+            cv_psum = bank(g, [P, 2, B_TILES, P], F32, "cv_psum")
             for c in range(B_TILES):
-                nc.sync.dma_start(out=cv_rows[:, c, :], in_=cv_dram[:, c, :])
-            adj_rows = setup.tile([P, D * D], BF16)
-            nc.scalar.dma_start(out=adj_rows[:], in_=adj_soft.rearrange("i j -> (i j)").partition_broadcast(P))
-            b1_rows = setup.tile([P, P], BF16)
-            nc.vector.memset(b1_rows[:], 0.0)
-            nc.scalar.dma_start(out=b1_rows[0 : D * H_TILES, :], in_=b1.rearrange("i (c m) -> (i c) m", m=P))
-            nc.vector.memset(w1_planes[:].bitcast(I32), 0)
-            nc.vector.memset(w2_planes[:].bitcast(I32), 0)
-            nc.vector.memset(minus_half[:], -0.5)
-
-            load_w1_planes(0, FIRST_PLANES)
-            for i in range(FIRST_PLANES):
-                load_w1_words(i)
-            for quadrant in range(P // QUADRANT):
-                nc.sync.dma_start(
-                    out=w2_planes[QUADRANT * quadrant : QUADRANT * quadrant + LIVE, :, :].bitcast(I32),
-                    in_=w2_scales_dram[LIVE * quadrant : LIVE * (quadrant + 1), :, :],
-                )
-            nc.sync.dma_start(out=w2_words[:], in_=w2_words_dram)
-            load_w1_planes(FIRST_PLANES, D - FIRST_PLANES)
-            load_w1_words(FIRST_PLANES)
-            nc.sync.dma_start(out=b2_rows[:], in_=b2.rearrange("i v -> (i v)").partition_broadcast(P))
-            nc.sync.dma_start(out=gamma_rows[:], in_=gamma.rearrange("i v -> (i v)").partition_broadcast(P))
-            nc.sync.dma_start(out=beta_rows[:], in_=beta.rearrange("i v -> (i v)").partition_broadcast(P))
-            for i in range(FIRST_PLANES + 1, D):
-                load_w1_words(i)
-
-            make_identity(nc, ident_f32[:])
-            make_identity(nc, ident_bf16[:])
-
-            adj_by_quadrant = adj_rows[:].rearrange("p (i g q) -> p i g q", g=PASSES, q=P // QUADRANT)
-            for quadrant in range(P // QUADRANT):
-                rows = slice(QUADRANT * quadrant, QUADRANT * (quadrant + 1))
-                nc.vector.tensor_copy(out=adj_col[rows, :, :], in_=adj_by_quadrant[rows, :, :, quadrant])
-
-            b1_psum = setup_psum.tile([P, P], BF16)
-            nc.tensor.transpose(b1_psum[:], b1_rows[:], ident_bf16[:])
-            nc.vector.tensor_copy(out=b1_col[:], in_=b1_psum[:, 0 : D * H_TILES])
-
-            for g in range(PASSES):
-                cv_psum = setup_psum.tile([P, 2, B_TILES, P], F32, name="cv_psum%d" % g)
-                for c in range(B_TILES):
-                    words = cv_rows[:, c, :].bitcast(F32)
-                    for u in range(2):
-                        nc.tensor.transpose(
-                            cv_psum[:, u, c, :],
-                            words[:, 2 * P * g + u : 2 * P * (g + 1) : 2],
-                            ident_f32[:],
-                        )
-                copy = nc.vector.tensor_copy if g % 2 == 0 else nc.scalar.copy
-                copy(
-                    out=cv_mx[:, B * PACK * g : B * PACK * (g + 1)].bitcast(F32).rearrange("p (b u) -> p b u", u=2),
-                    in_=cv_psum[:].rearrange("p u c b -> p (c b) u"),
-                )
-
-        with tc.tile_pool(name="work", bufs=2) as work, tc.psum_pool(name="psum", bufs=1) as psum:
-            live = {}
-
-            def scale_x(i):
-                x = work.tile([P, PASSES * B * PACK], BF16, name="x", align_bytes=64)
-                for g in range(PASSES):
-                    cols = slice(B * PACK * g, B * PACK * (g + 1))
-                    nc.vector.tensor_scalar_mul(out=x[:, cols], in0=cv_mx[:, cols], scalar1=adj_col[:, i, g : g + 1])
-                live["x", i] = x
-
-            def quantise_x(i):
-                x_codes = work.tile([P, PASSES * B], U32, name="x_codes", bufs=3, align_bytes=64)
-                x_plane = work.tile([P, PASSES * B], U8, name="x_plane", bufs=3, align_bytes=64)
-                nc.vector.quantize_mx(out=x_codes[:].bitcast(FP8X4), scales=x_plane[:], in_=live["x", i][:])
-                live["x_codes", i] = x_codes
-                live["x_plane", i] = x_plane
-
-            def layer1(i):
-                x_codes = live["x_codes", i]
-                x_plane = live["x_plane", i]
-                for half in range(2):
-                    h_psum = psum.tile([P, 2, B], F32, name="h_psum%d" % half, bufs=2)
-                    for c2 in range(2):
-                        n_cols = slice(P * (2 * half + c2), P * (2 * half + c2 + 1))
-                        for g in range(PASSES):
-                            b_cols = slice(B * g, B * (g + 1))
-                            nc.tensor.matmul_mx(
-                                out=h_psum[:, c2, :],
-                                lhsT=w1_words[i][:, g, n_cols].bitcast(FP8X4),
-                                lhsT_scale=w1_planes[LIVE * g : P, i, n_cols],
-                                rhs=x_codes[:, b_cols].bitcast(FP8X4),
-                                rhs_scale=x_plane[:, b_cols],
-                                start=(g == 0),
-                                stop=(g == PASSES - 1),
-                            )
-                    live["h_psum", i, half] = h_psum
-
-            def gelu(i):
-                h_cols = work.tile([P, H_TILES, B], BF16, name="h_cols")
-                for c in range(H_TILES):
-                    nc.scalar.activation(
-                        out=h_cols[:, c, :],
-                        in_=live["h_psum", i, c // 2][:, c % 2, :],
-                        func=ACT.Gelu,
-                        bias=b1_col[:, H_TILES * i + c : H_TILES * i + c + 1],
-                        scale=1.0,
-                    )
-                live["h_cols", i] = h_cols
-
-            def rows_of_h(i):
-                h_cols = live["h_cols", i]
-                h_rows_psum = psum.tile([P, B_TILES, H], BF16, name="h_rows_psum")
-                for c in range(H_TILES):
-                    for bt in range(B_TILES):
-                        nc.tensor.transpose(
-                            h_rows_psum[:, bt, P * c : P * (c + 1)], h_cols[:, c, P * bt : P * (bt + 1)], ident_bf16[:]
-                        )
-                live["h_rows_psum", i] = h_rows_psum
-
-            def sort_words(i):
-                h_rows = work.tile([P, B_TILES, 2, P], F32, name="h_rows")
-                nc.scalar.copy(
-                    out=h_rows[:],
-                    in_=live["h_rows_psum", i][:].bitcast(F32).rearrange("b c (p u) -> b c u p", u=2),
-                )
-                live["h_rows", i] = h_rows
-
-            def words_of_h(i):
-                h_rows = live["h_rows", i]
-                h_words_psum = psum.tile([P, 2, B_TILES, P], F32, name="h_words_psum")
+                words = cv_rows[:, c, :].bitcast(F32)
                 for u in range(2):
-                    for bt in range(B_TILES):
-                        nc.tensor.transpose(h_words_psum[:, u, bt, :], h_rows[:, bt, u, :], ident_f32[:])
-                live["h_words_psum", i] = h_words_psum
+                    nc.tensor.transpose(cv_psum[:, u, c, :], words[:, 2 * P * g + u : 2 * P * (g + 1) : 2], ident_f32[:])
+            copy = nc.vector.tensor_copy if g % 2 == 0 else nc.scalar.copy
+            copy(
+                out=cv_mx[:, B * PACK * g : B * PACK * (g + 1)].bitcast(F32).rearrange("p (b u) -> p b u", u=2),
+                in_=cv_psum[:].rearrange("p u c b -> p (c b) u"),
+            )
 
-            def interleave(i):
-                h_mx = work.tile([P, B * PACK], BF16, name="h_mx", align_bytes=64)
-                nc.scalar.copy(
-                    out=h_mx[:].bitcast(F32).rearrange("p (b u) -> p b u", u=2),
-                    in_=live["h_words_psum", i][:].rearrange("p u c b -> p (c b) u"),
+        for r, repeated in enumerate((b2_rows, gamma_rows, beta_rows)):
+            for j in range(D * V // BANK):
+                cols = slice(BANK * j, BANK * (j + 1))
+                vector_psum = bank(4 + j, [P, BANK], F32, "vector_psum")
+                nc.tensor.matmul(vector_psum[:], lhsT=select[:, r, :], rhs=vectors[:, cols], start=True, stop=True)
+                nc.scalar.copy(out=repeated[:, cols], in_=vector_psum[:])
+
+        live = {}
+
+        def scale_x(i):
+            x = work.tile([P, PASSES * B * PACK], BF16, name="x", bufs=1, align_bytes=64)
+            for g in range(PASSES):
+                cols = slice(B * PACK * g, B * PACK * (g + 1))
+                nc.vector.tensor_scalar_mul(out=x[:, cols], in0=cv_mx[:, cols], scalar1=adj_col[:, i, g : g + 1])
+            live["x", i] = x
+
+        def quantise_x(i):
+            x_codes = work.tile([P, PASSES * B], U32, name="x_codes", bufs=3, align_bytes=64)
+            x_plane = work.tile([P, PASSES * B], U8, name="x_plane", bufs=3, align_bytes=64)
+            nc.vector.quantize_mx(out=x_codes[:].bitcast(FP8X4), scales=x_plane[:], in_=live["x", i][:])
+            live["x_codes", i] = x_codes
+            live["x_plane", i] = x_plane
+
+        def layer1(i):
+            x_codes = live["x_codes", i]
+            x_plane = live["x_plane", i]
+            for half in range(2):
+                h_psum = bank(2 * (i % 2) + half, [P, 2, B], F32, "h_psum")
+                for c2 in range(2):
+                    n_cols = slice(P * (2 * half + c2), P * (2 * half + c2 + 1))
+                    for g in range(PASSES):
+                        b_cols = slice(B * g, B * (g + 1))
+                        nc.tensor.matmul_mx(
+                            out=h_psum[:, c2, :],
+                            lhsT=w1_words[i][:, g, n_cols].bitcast(FP8X4),
+                            lhsT_scale=w1_planes[LIVE * g : P, i, n_cols],
+                            rhs=x_codes[:, b_cols].bitcast(FP8X4),
+                            rhs_scale=x_plane[:, b_cols],
+                            start=(g == 0),
+                            stop=(g == PASSES - 1),
+                        )
+                live["h_psum", i, half] = h_psum
+
+        def gelu(i):
+            h_cols = work.tile([P, H_TILES, B], BF16, name="h_cols")
+            for c in range(H_TILES):
+                nc.scalar.activation(
+                    out=h_cols[:, c, :],
+                    in_=live["h_psum", i, c // 2][:, c % 2, :],
+                    func=ACT.Gelu,
+                    bias=b1_col[:, H_TILES * i + c : H_TILES * i + c + 1],
+                    scale=1.0,
                 )
-                live["h_mx", i] = h_mx
+            live["h_cols", i] = h_cols
 
-            def quantise_h(i):
-                h_codes = work.tile([P, B], U32, name="h_codes", align_bytes=64)
-                h_plane = work.tile([P, B], U8, name="h_plane", align_bytes=64)
-                nc.vector.quantize_mx(out=h_codes[:].bitcast(FP8X4), scales=h_plane[:], in_=live["h_mx", i][:])
-                live["h_codes", i] = h_codes
-                live["h_plane", i] = h_plane
-
-            def layer2(i):
-                h_codes = live["h_codes", i]
-                h_plane = live["h_plane", i]
-                y_psum = psum.tile([P, B_TILES, V], F32, name="y_psum", bufs=2)
+        def rows_of_h(i):
+            h_cols = live["h_cols", i]
+            h_rows_psum = bank(4, [P, B_TILES, H], BF16, "h_rows_psum")
+            for c in range(H_TILES):
                 for bt in range(B_TILES):
-                    b_cols = slice(P * bt, P * (bt + 1))
-                    nc.tensor.matmul_mx(
-                        out=y_psum[:, bt, :],
-                        lhsT=h_codes[:, b_cols].bitcast(FP8X4),
-                        lhsT_scale=h_plane[:, b_cols],
-                        rhs=w2_words[:, i, :].bitcast(FP8X4),
-                        rhs_scale=w2_planes[:, i, :],
-                        start=True,
-                        stop=True,
+                    nc.tensor.transpose(
+                        h_rows_psum[:, bt, P * c : P * (c + 1)], h_cols[:, c, P * bt : P * (bt + 1)], ident_bf16[:]
                     )
-                live["y_psum", i] = y_psum
+            live["h_rows_psum", i] = h_rows_psum
 
-            def norm_mean(i):
-                y_psum = live["y_psum", i]
-                y = work.tile([P, B_TILES, V], F32, name="y")
-                y_sum = work.tile([P, B_TILES], F32, name="y_sum", bufs=3)
-                minus_mean = work.tile([P, B_TILES], F32, name="minus_mean", bufs=3)
+        def sort_words(i):
+            h_rows = work.tile([P, B_TILES, 2, P], F32, name="h_rows")
+            nc.scalar.copy(
+                out=h_rows[:],
+                in_=live["h_rows_psum", i][:].bitcast(F32).rearrange("b c (p u) -> b c u p", u=2),
+            )
+            live["h_rows", i] = h_rows
+
+        def words_of_h(i):
+            h_rows = live["h_rows", i]
+            h_words_psum = bank(5, [P, 2, B_TILES, P], F32, "h_words_psum")
+            for u in range(2):
                 for bt in range(B_TILES):
-                    nc.vector.scalar_tensor_tensor(
-                        out=y[:, bt, :],
-                        in0=y_psum[:, bt, :],
-                        scalar=1.0,
-                        in1=b2_rows[:, V * i : V * (i + 1)],
-                        op0=ALU.mult,
-                        op1=ALU.add,
-                        accum_out=y_sum[:, bt : bt + 1],
-                    )
-                nc.gpsimd.tensor_scalar(
-                    out=minus_mean[:], in0=y_sum[:], scalar1=-1.0 / V, scalar2=0.0, op0=ALU.mult, op1=ALU.add
+                    nc.tensor.transpose(h_words_psum[:, u, bt, :], h_rows[:, bt, u, :], ident_f32[:])
+            live["h_words_psum", i] = h_words_psum
+
+        def interleave(i):
+            h_mx = work.tile([P, B * PACK], BF16, name="h_mx", align_bytes=64)
+            nc.scalar.copy(
+                out=h_mx[:].bitcast(F32).rearrange("p (b u) -> p b u", u=2),
+                in_=live["h_words_psum", i][:].rearrange("p u c b -> p (c b) u"),
+            )
+            live["h_mx", i] = h_mx
+
+        def quantise_h(i):
+            h_codes = work.tile([P, B], U32, name="h_codes", align_bytes=64)
+            h_plane = work.tile([P, B], U8, name="h_plane", align_bytes=64)
+            nc.vector.quantize_mx(out=h_codes[:].bitcast(FP8X4), scales=h_plane[:], in_=live["h_mx", i][:])
+            live["h_codes", i] = h_codes
+            live["h_plane", i] = h_plane
+
+        def layer2(i):
+            h_codes = live["h_codes", i]
+            h_plane = live["h_plane", i]
+            y_psum = bank(6 + i % 2, [P, B_TILES, V], F32, "y_psum")
+            for bt in range(B_TILES):
+                b_cols = slice(P * bt, P * (bt + 1))
+                nc.tensor.matmul_mx(
+                    out=y_psum[:, bt, :],
+                    lhsT=h_codes[:, b_cols].bitcast(FP8X4),
+                    lhsT_scale=h_plane[:, b_cols],
+                    rhs=w2_words[:, i, :].bitcast(FP8X4),
+                    rhs_scale=w2_planes[:, i, :],
+                    start=True,
+                    stop=True,
                 )
-                live["y", i] = y
-                live["minus_mean", i] = minus_mean
+            live["y_psum", i] = y_psum
 
-            def norm_variance(i):
-                y = live["y", i]
-                minus_mean = live["minus_mean", i]
-                squares = work.tile([P, V], BF16, name="squares")
-                square_sum = work.tile([P, B_TILES], F32, name="square_sum", bufs=3)
-                var_eps = work.tile([P, B_TILES], F32, name="var_eps", bufs=3)
-                rstd = work.tile([P, B_TILES], F32, name="rstd", bufs=3)
-                for bt in range(B_TILES):
-                    nc.scalar.activation(
-                        out=squares[:],
-                        in_=y[:, bt, :],
-                        func=ACT.Square,
-                        bias=minus_mean[:, bt : bt + 1],
-                        scale=1.0,
-                        accum_out=square_sum[:, bt : bt + 1],
-                    )
-                nc.gpsimd.tensor_scalar(
-                    out=var_eps[:], in0=square_sum[:], scalar1=1.0 / V, scalar2=LN_EPS, op0=ALU.mult, op1=ALU.add
+        def norm_mean(i):
+            y_psum = live["y_psum", i]
+            y = work.tile([P, B_TILES, V], F32, name="y")
+            y_sum = work.tile([P, B_TILES], F32, name="y_sum", bufs=3)
+            minus_mean = work.tile([P, B_TILES], F32, name="minus_mean", bufs=3)
+            for bt in range(B_TILES):
+                nc.vector.scalar_tensor_tensor(
+                    out=y[:, bt, :],
+                    in0=y_psum[:, bt, :],
+                    scalar=1.0,
+                    in1=b2_rows[:, V * i : V * (i + 1)],
+                    op0=ALU.mult,
+                    op1=ALU.add,
+                    accum_out=y_sum[:, bt : bt + 1],
                 )
-                nc.gpsimd.tensor_tensor(out=rstd[:], in0=var_eps[:], in1=minus_half[:], op=ALU.pow)
-                live["rstd", i] = rstd
+            nc.gpsimd.tensor_scalar(
+                out=minus_mean[:], in0=y_sum[:], scalar1=-1.0 / V, scalar2=0.0, op0=ALU.mult, op1=ALU.add
+            )
+            live["y", i] = y
+            live["minus_mean", i] = minus_mean
 
-            def norm_gain(i):
-                y = live["y", i]
-                minus_mean = live["minus_mean", i]
-                centred = work.tile([P, B_TILES, V], F32, name="centred")
-                for bt in range(B_TILES):
-                    nc.vector.scalar_tensor_tensor(
-                        out=centred[:, bt, :],
-                        in0=y[:, bt, :],
-                        scalar=minus_mean[:, bt : bt + 1],
-                        in1=gamma_rows[:, V * i : V * (i + 1)],
-                        op0=ALU.add,
-                        op1=ALU.mult,
-                    )
-                live["centred", i] = centred
+        def norm_variance(i):
+            y = live["y", i]
+            minus_mean = live["minus_mean", i]
+            squares = work.tile([P, V], BF16, name="squares")
+            square_sum = work.tile([P, B_TILES], F32, name="square_sum", bufs=3)
+            var_eps = work.tile([P, B_TILES], F32, name="var_eps", bufs=3)
+            rstd = work.tile([P, B_TILES], F32, name="rstd", bufs=3)
+            for bt in range(B_TILES):
+                nc.scalar.activation(
+                    out=squares[:],
+                    in_=y[:, bt, :],
+                    func=ACT.Square,
+                    bias=minus_mean[:, bt : bt + 1],
+                    scale=1.0,
+                    accum_out=square_sum[:, bt : bt + 1],
+                )
+            nc.gpsimd.tensor_scalar(
+                out=var_eps[:], in0=square_sum[:], scalar1=1.0 / V, scalar2=LN_EPS, op0=ALU.mult, op1=ALU.add
+            )
+            nc.gpsimd.tensor_tensor(out=rstd[:], in0=var_eps[:], in1=minus_half[:], op=ALU.pow)
+            live["rstd", i] = rstd
 
-            def norm_shift_and_store(i):
-                centred = live["centred", i]
-                rstd = live["rstd", i]
-                result = work.tile([P, B_TILES, V], F32, name="result", bufs=3)
-                for bt in range(B_TILES):
-                    nc.vector.scalar_tensor_tensor(
-                        out=result[:, bt, :],
-                        in0=centred[:, bt, :],
-                        scalar=rstd[:, bt : bt + 1],
-                        in1=beta_rows[:, V * i : V * (i + 1)],
-                        op0=ALU.mult,
-                        op1=ALU.add,
-                    )
-                nc.sync.dma_start(out=out_dram[:, :, i, :], in_=result[:])
+        def norm_gain(i):
+            y = live["y", i]
+            minus_mean = live["minus_mean", i]
+            centred = work.tile([P, B_TILES, V], F32, name="centred")
+            for bt in range(B_TILES):
+                nc.vector.scalar_tensor_tensor(
+                    out=centred[:, bt, :],
+                    in0=y[:, bt, :],
+                    scalar=minus_mean[:, bt : bt + 1],
+                    in1=gamma_rows[:, V * i : V * (i + 1)],
+                    op0=ALU.add,
+                    op1=ALU.mult,
+                )
+            live["centred", i] = centred
 
-            def run(stage, i):
-                if 0 <= i < D:
-                    stage(i)
+        def norm_shift_and_store(i):
+            centred = live["centred", i]
+            rstd = live["rstd", i]
+            result = work.tile([P, B_TILES, V], F32, name="result", bufs=3)
+            for bt in range(B_TILES):
+                nc.vector.scalar_tensor_tensor(
+                    out=result[:, bt, :],
+                    in0=centred[:, bt, :],
+                    scalar=rstd[:, bt : bt + 1],
+                    in1=beta_rows[:, V * i : V * (i + 1)],
+                    op0=ALU.mult,
+                    op1=ALU.add,
+                )
+            nc.sync.dma_start(out=out_dram[:, :, i, :], in_=result[:])
 
-            with tc.manual_schedule():
-                for i in range(2):
-                    scale_x(i)
-                    quantise_x(i)
-                for s in range(D + 6):
-                    run(norm_shift_and_store, s - 5)
-                    run(sort_words, s - 2)
-                    run(norm_mean, s - 4)
-                    run(gelu, s - 1)
-                    run(scale_x, s + 2)
-                    run(interleave, s - 3)
-                    run(norm_gain, s - 4)
-                    run(norm_variance, s - 4)
-                    run(quantise_h, s - 3)
-                    run(quantise_x, s + 2)
-                    run(layer1, s)
-                    run(words_of_h, s - 2)
-                    run(rows_of_h, s - 1)
-                    run(layer2, s - 3)
+        def run(stage, i):
+            if 0 <= i < D:
+                stage(i)
+
+        for i in range(2):
+            scale_x(i)
+            quantise_x(i)
+        for s in range(D + 6):
+            run(norm_shift_and_store, s - 5)
+            run(load_equation, s + LOOKAHEAD)
+            run(sort_words, s - 2)
+            run(norm_mean, s - 4)
+            run(gelu, s - 1)
+            run(scale_x, s + 2)
+            run(interleave, s - 3)
+            run(norm_gain, s - 4)
+            run(norm_variance, s - 4)
+            run(quantise_h, s - 3)
+            run(quantise_x, s + 2)
+            run(layer1, s)
+            run(words_of_h, s - 2)
+            run(rows_of_h, s - 1)
+            run(layer2, s - 3)

@@ -65,7 +65,7 @@ def tile_structuralequationmodels_e_kernel(
         b2_rows = keep.tile([P, D * V], BF16)
         gamma_rows = keep.tile([P, D * V], BF16)
         beta_rows = keep.tile([P, D * V], BF16)
-        cv_rows = keep.tile([P, B_TILES, K], BF16)
+        cv_rows = keep.tile([P, PASSES, B_TILES, K_PASS], BF16)
         vectors = keep.tile([P, D * V], BF16)
         select = keep.tile([P, QUADRANTS, P], BF16)
         b1_rows = keep.tile([P, P], BF16)
@@ -82,8 +82,8 @@ def tile_structuralequationmodels_e_kernel(
                         )
             nc.sync.dma_start(out=w1_words[i][:], in_=w1_words_dram[:, PASSES * i : PASSES * (i + 1), :])
 
-        for c in range(B_TILES):
-            nc.sync.dma_start(out=cv_rows[:, c, :], in_=cv_dram[:, c, :])
+        for g in range(PASSES):
+            nc.sync.dma_start(out=cv_rows[:, g, :, :], in_=cv_dram[:, :, K_PASS * g : K_PASS * (g + 1)])
         nc.vector.memset(vectors[:], 0.0)
         nc.vector.memset(b1_rows[:], 0.0)
         nc.vector.memset(select[:], 0.0)
@@ -93,7 +93,8 @@ def tile_structuralequationmodels_e_kernel(
             row = vector.rearrange("i v -> (i v)").unsqueeze(0)
             nc.scalar.dma_start(out=vectors[QUADRANT * r : QUADRANT * r + 1, 0 : row.shape[1]], in_=row)
         nc.scalar.dma_start(out=b1_rows[0 : D * H_TILES, :], in_=b1.rearrange("i (c m) -> (i c) m", m=P))
-        nc.vector.memset(w1_planes[:].bitcast(I32), 0)
+        for i in range(0, D, PLANE_GROUP):
+            nc.vector.memset(w1_planes[:, i : i + PLANE_GROUP, :].bitcast(I32), 0)
         nc.vector.memset(w2_planes[:].bitcast(I32), 0)
         for i in range(LOOKAHEAD):
             load_equation(i)
@@ -108,6 +109,20 @@ def tile_structuralequationmodels_e_kernel(
         make_identity(nc, ident_f32[:])
         make_identity(nc, ident_bf16[:])
 
+        def repeat_on_all_partitions(r, repeated, first_bank):
+            for j in range(D * V // (2 * BANK)):
+                vector_psum = bank(first_bank + j, [P, 2 * BANK], BF16, "vector_psum")
+                for half in range(2):
+                    cols = slice(BANK * half, BANK * (half + 1))
+                    nc.tensor.matmul(
+                        vector_psum[:, cols],
+                        lhsT=select[:, r, :],
+                        rhs=vectors[:, 2 * BANK * j + BANK * half : 2 * BANK * j + BANK * (half + 1)],
+                        start=True,
+                        stop=True,
+                    )
+                nc.scalar.copy(out=repeated[:, 2 * BANK * j : 2 * BANK * (j + 1)], in_=vector_psum[:])
+
         adj_psum = bank(4, [P, D * D], F32, "adj_psum")
         nc.tensor.matmul(adj_psum[:], lhsT=select[:, 3, :], rhs=vectors[:, 0 : D * D], start=True, stop=True)
         adj_by_quadrant = adj_psum[:].rearrange("p (i g q) -> p i g q", g=PASSES, q=QUADRANTS)
@@ -119,24 +134,22 @@ def tile_structuralequationmodels_e_kernel(
         nc.tensor.transpose(b1_psum[:], b1_rows[:], ident_bf16[:])
         nc.vector.tensor_copy(out=b1_col[:], in_=b1_psum[:, 0 : D * H_TILES])
 
+        repeat_on_all_partitions(0, b2_rows, 6)
+
         for g in range(PASSES):
             cv_psum = bank(g, [P, 2, B_TILES, P], F32, "cv_psum")
             for c in range(B_TILES):
-                words = cv_rows[:, c, :].bitcast(F32)
+                words = cv_rows[:, g, c, :].bitcast(F32)
                 for u in range(2):
-                    nc.tensor.transpose(cv_psum[:, u, c, :], words[:, 2 * P * g + u : 2 * P * (g + 1) : 2], ident_f32[:])
+                    nc.tensor.transpose(cv_psum[:, u, c, :], words[:, u : 2 * P : 2], ident_f32[:])
             copy = nc.vector.tensor_copy if g % 2 == 0 else nc.scalar.copy
             copy(
                 out=cv_mx[:, B * PACK * g : B * PACK * (g + 1)].bitcast(F32).rearrange("p (b u) -> p b u", u=2),
                 in_=cv_psum[:].rearrange("p u c b -> p (c b) u"),
             )
 
-        for r, repeated in enumerate((b2_rows, gamma_rows, beta_rows)):
-            for j in range(D * V // BANK):
-                cols = slice(BANK * j, BANK * (j + 1))
-                vector_psum = bank(4 + j, [P, BANK], F32, "vector_psum")
-                nc.tensor.matmul(vector_psum[:], lhsT=select[:, r, :], rhs=vectors[:, cols], start=True, stop=True)
-                nc.scalar.copy(out=repeated[:, cols], in_=vector_psum[:])
+        repeat_on_all_partitions(1, gamma_rows, 4)
+        repeat_on_all_partitions(2, beta_rows, 6)
 
         live = {}
 
@@ -246,9 +259,8 @@ def tile_structuralequationmodels_e_kernel(
 
         def norm_mean(i):
             y_psum = live["y_psum", i]
-            y = work.tile([P, B_TILES, V], F32, name="y")
+            y = work.tile([P, B_TILES, V], F32, name="y", bufs=3)
             y_sum = work.tile([P, B_TILES], F32, name="y_sum", bufs=3)
-            minus_mean = work.tile([P, B_TILES], F32, name="minus_mean", bufs=3)
             for bt in range(B_TILES):
                 nc.vector.scalar_tensor_tensor(
                     out=y[:, bt, :],
@@ -259,19 +271,17 @@ def tile_structuralequationmodels_e_kernel(
                     op1=ALU.add,
                     accum_out=y_sum[:, bt : bt + 1],
                 )
-            nc.gpsimd.tensor_scalar(
-                out=minus_mean[:], in0=y_sum[:], scalar1=-1.0 / V, scalar2=0.0, op0=ALU.mult, op1=ALU.add
-            )
             live["y", i] = y
-            live["minus_mean", i] = minus_mean
+            live["y_sum", i] = y_sum
 
         def norm_variance(i):
             y = live["y", i]
-            minus_mean = live["minus_mean", i]
+            minus_mean = work.tile([P, B_TILES], F32, name="minus_mean", bufs=3)
             squares = work.tile([P, V], BF16, name="squares")
             square_sum = work.tile([P, B_TILES], F32, name="square_sum", bufs=3)
             var_eps = work.tile([P, B_TILES], F32, name="var_eps", bufs=3)
-            rstd = work.tile([P, B_TILES], F32, name="rstd", bufs=3)
+            rstd = work.tile([P, B_TILES], F32, name="rstd", bufs=5)
+            nc.scalar.mul(out=minus_mean[:], in_=live["y_sum", i][:], mul=-1.0 / V)
             for bt in range(B_TILES):
                 nc.scalar.activation(
                     out=squares[:],
@@ -285,12 +295,13 @@ def tile_structuralequationmodels_e_kernel(
                 out=var_eps[:], in0=square_sum[:], scalar1=1.0 / V, scalar2=LN_EPS, op0=ALU.mult, op1=ALU.add
             )
             nc.gpsimd.tensor_tensor(out=rstd[:], in0=var_eps[:], in1=minus_half[:], op=ALU.pow)
+            live["minus_mean", i] = minus_mean
             live["rstd", i] = rstd
 
         def norm_gain(i):
             y = live["y", i]
             minus_mean = live["minus_mean", i]
-            centred = work.tile([P, B_TILES, V], F32, name="centred")
+            centred = work.tile([P, B_TILES, V], F32, name="centred", bufs=4)
             for bt in range(B_TILES):
                 nc.vector.scalar_tensor_tensor(
                     out=centred[:, bt, :],
@@ -324,18 +335,18 @@ def tile_structuralequationmodels_e_kernel(
         for i in range(2):
             scale_x(i)
             quantise_x(i)
-        for s in range(D + 6):
-            run(norm_shift_and_store, s - 5)
+        for s in range(D + 9):
+            run(norm_shift_and_store, s - 8)
             run(load_equation, s + LOOKAHEAD)
-            run(sort_words, s - 2)
-            run(norm_mean, s - 4)
             run(gelu, s - 1)
+            run(norm_mean, s - 5)
+            run(sort_words, s - 2)
             run(scale_x, s + 2)
             run(interleave, s - 3)
-            run(norm_gain, s - 4)
-            run(norm_variance, s - 4)
-            run(quantise_h, s - 3)
+            run(norm_gain, s - 6)
+            run(norm_variance, s - 5)
             run(quantise_x, s + 2)
+            run(quantise_h, s - 3)
             run(layer1, s)
             run(words_of_h, s - 2)
             run(rows_of_h, s - 1)

@@ -27,6 +27,7 @@ BANK = 512
 LN_EPS = 1e-5
 PLANE_GROUP = 4
 LOOKAHEAD = 4
+STORE_GROUP = 2
 
 FLOPS = 2 * B * D * (K * H + H * V)
 
@@ -81,30 +82,31 @@ def tile_structuralequationmodels_e_kernel(
                             in_=w1_scales_dram[:, LIVE * quadrant + r, group, :],
                         )
             nc.sync.dma_start(out=w1_words[i][:], in_=w1_words_dram[:, PASSES * i : PASSES * (i + 1), :])
+            nc.sync.dma_start(out=w2_words[:, i, :], in_=w2_words_dram[:, i, :])
 
         for g in range(PASSES):
             nc.sync.dma_start(out=cv_rows[:, g, :, :], in_=cv_dram[:, :, K_PASS * g : K_PASS * (g + 1)])
         nc.vector.memset(vectors[:], 0.0)
-        nc.vector.memset(b1_rows[:], 0.0)
-        nc.vector.memset(select[:], 0.0)
-        for r in range(QUADRANTS):
-            nc.vector.memset(select[QUADRANT * r : QUADRANT * r + 1, r, :], 1.0)
         for r, vector in enumerate((b2, gamma, beta, adj_soft)):
             row = vector.rearrange("i v -> (i v)").unsqueeze(0)
             nc.scalar.dma_start(out=vectors[QUADRANT * r : QUADRANT * r + 1, 0 : row.shape[1]], in_=row)
+        nc.vector.memset(b1_rows[:], 0.0)
         nc.scalar.dma_start(out=b1_rows[0 : D * H_TILES, :], in_=b1.rearrange("i (c m) -> (i c) m", m=P))
         for i in range(0, D, PLANE_GROUP):
             nc.vector.memset(w1_planes[:, i : i + PLANE_GROUP, :].bitcast(I32), 0)
         nc.vector.memset(w2_planes[:].bitcast(I32), 0)
-        for i in range(LOOKAHEAD):
-            load_equation(i)
+        load_equation(0)
         for quadrant in range(QUADRANTS):
             nc.sync.dma_start(
                 out=w2_planes[QUADRANT * quadrant : QUADRANT * quadrant + LIVE, :, :].bitcast(I32),
                 in_=w2_scales_dram[LIVE * quadrant : LIVE * (quadrant + 1), :, :],
             )
-        nc.sync.dma_start(out=w2_words[:], in_=w2_words_dram)
+        for i in range(1, LOOKAHEAD):
+            load_equation(i)
 
+        nc.vector.memset(select[:], 0.0)
+        for r in range(QUADRANTS):
+            nc.vector.memset(select[QUADRANT * r : QUADRANT * r + 1, r, :], 1.0)
         nc.vector.memset(minus_half[:], -0.5)
         make_identity(nc, ident_f32[:])
         make_identity(nc, ident_bf16[:])
@@ -123,19 +125,6 @@ def tile_structuralequationmodels_e_kernel(
                     )
                 nc.scalar.copy(out=repeated[:, 2 * BANK * j : 2 * BANK * (j + 1)], in_=vector_psum[:])
 
-        adj_psum = bank(4, [P, D * D], F32, "adj_psum")
-        nc.tensor.matmul(adj_psum[:], lhsT=select[:, 3, :], rhs=vectors[:, 0 : D * D], start=True, stop=True)
-        adj_by_quadrant = adj_psum[:].rearrange("p (i g q) -> p i g q", g=PASSES, q=QUADRANTS)
-        for quadrant in range(QUADRANTS):
-            rows = slice(QUADRANT * quadrant, QUADRANT * (quadrant + 1))
-            nc.vector.tensor_copy(out=adj_col[rows, :, :], in_=adj_by_quadrant[rows, :, :, quadrant])
-
-        b1_psum = bank(5, [P, P], BF16, "b1_psum")
-        nc.tensor.transpose(b1_psum[:], b1_rows[:], ident_bf16[:])
-        nc.vector.tensor_copy(out=b1_col[:], in_=b1_psum[:, 0 : D * H_TILES])
-
-        repeat_on_all_partitions(0, b2_rows, 6)
-
         for g in range(PASSES):
             cv_psum = bank(g, [P, 2, B_TILES, P], F32, "cv_psum")
             for c in range(B_TILES):
@@ -148,6 +137,18 @@ def tile_structuralequationmodels_e_kernel(
                 in_=cv_psum[:].rearrange("p u c b -> p (c b) u"),
             )
 
+        adj_psum = bank(4, [P, D * D], F32, "adj_psum")
+        nc.tensor.matmul(adj_psum[:], lhsT=select[:, 3, :], rhs=vectors[:, 0 : D * D], start=True, stop=True)
+        adj_by_quadrant = adj_psum[:].rearrange("p (i g q) -> p i g q", g=PASSES, q=QUADRANTS)
+        for quadrant in range(QUADRANTS):
+            rows = slice(QUADRANT * quadrant, QUADRANT * (quadrant + 1))
+            nc.vector.tensor_copy(out=adj_col[rows, :, :], in_=adj_by_quadrant[rows, :, :, quadrant])
+
+        b1_psum = bank(5, [P, P], BF16, "b1_psum")
+        nc.tensor.transpose(b1_psum[:], b1_rows[:], ident_bf16[:])
+        nc.vector.tensor_copy(out=b1_col[:], in_=b1_psum[:, 0 : D * H_TILES])
+
+        repeat_on_all_partitions(0, b2_rows, 6)
         repeat_on_all_partitions(1, gamma_rows, 4)
         repeat_on_all_partitions(2, beta_rows, 6)
 
@@ -316,17 +317,21 @@ def tile_structuralequationmodels_e_kernel(
         def norm_shift_and_store(i):
             centred = live["centred", i]
             rstd = live["rstd", i]
-            result = work.tile([P, B_TILES, V], F32, name="result", bufs=3)
+            first = i - i % STORE_GROUP
+            if i == first:
+                live["result", first] = work.tile([P, B_TILES, STORE_GROUP, V], F32, name="result", bufs=3)
+            result = live["result", first]
             for bt in range(B_TILES):
                 nc.vector.scalar_tensor_tensor(
-                    out=result[:, bt, :],
+                    out=result[:, bt, i - first, :],
                     in0=centred[:, bt, :],
                     scalar=rstd[:, bt : bt + 1],
                     in1=beta_rows[:, V * i : V * (i + 1)],
                     op0=ALU.mult,
                     op1=ALU.add,
                 )
-            nc.sync.dma_start(out=out_dram[:, :, i, :], in_=result[:])
+            if i == first + STORE_GROUP - 1:
+                nc.sync.dma_start(out=out_dram[:, :, first : first + STORE_GROUP, :], in_=result[:])
 
         def run(stage, i):
             if 0 <= i < D:

@@ -25,9 +25,9 @@ QUADRANTS = P // QUADRANT
 LIVE = 4
 BANK = 512
 LN_EPS = 1e-5
-PLANE_GROUP = 4
+PLANE_GROUP = 8
 LOOKAHEAD = 4
-STORE_GROUP = 2
+PAIR = 2
 
 FLOPS = 2 * B * D * (K * H + H * V)
 
@@ -57,7 +57,8 @@ def tile_structuralequationmodels_e_kernel(
         ident_bf16 = keep.tile([P, P], BF16)
         adj_col = keep.tile([P, D, PASSES], F32)
         b1_col = keep.tile([P, D * H_TILES], F32)
-        minus_half = keep.tile([P, B_TILES], F32)
+        minus_half = keep.tile([P, PAIR * B_TILES], F32)
+        eps_col = keep.tile([P, 1], F32)
         cv_mx = keep.tile([P, PASSES * B * PACK], BF16, align_bytes=64)
         w1_words = [keep.tile([P, PASSES, H], I32, name="w1_words%d" % i, align_bytes=64) for i in range(D)]
         w1_planes = keep.tile([P, D, H], U8, align_bytes=64)
@@ -66,7 +67,7 @@ def tile_structuralequationmodels_e_kernel(
         b2_rows = keep.tile([P, D * V], BF16)
         gamma_rows = keep.tile([P, D * V], BF16)
         beta_rows = keep.tile([P, D * V], BF16)
-        cv_rows = keep.tile([P, PASSES, B_TILES, K_PASS], BF16)
+        cv_rows = work.tile([P, PASSES, B_TILES, K_PASS], BF16, name="cv_rows", tag="x", align_bytes=64)
         vectors = keep.tile([P, D * V], BF16)
         select = keep.tile([P, QUADRANTS, P], BF16)
         b1_rows = keep.tile([P, P], BF16)
@@ -108,6 +109,9 @@ def tile_structuralequationmodels_e_kernel(
         for r in range(QUADRANTS):
             nc.vector.memset(select[QUADRANT * r : QUADRANT * r + 1, r, :], 1.0)
         nc.vector.memset(minus_half[:], -0.5)
+        nc.vector.tensor_scalar(
+            out=eps_col[:], in0=minus_half[:, 0:1], scalar1=0.0, scalar2=LN_EPS, op0=ALU.mult, op1=ALU.add
+        )
         make_identity(nc, ident_f32[:])
         make_identity(nc, ident_bf16[:])
 
@@ -148,14 +152,10 @@ def tile_structuralequationmodels_e_kernel(
         nc.tensor.transpose(b1_psum[:], b1_rows[:], ident_bf16[:])
         nc.vector.tensor_copy(out=b1_col[:], in_=b1_psum[:, 0 : D * H_TILES])
 
-        repeat_on_all_partitions(0, b2_rows, 6)
-        repeat_on_all_partitions(1, gamma_rows, 4)
-        repeat_on_all_partitions(2, beta_rows, 6)
-
         live = {}
 
         def scale_x(i):
-            x = work.tile([P, PASSES * B * PACK], BF16, name="x", bufs=1, align_bytes=64)
+            x = work.tile([P, PASSES * B * PACK], BF16, name="x", tag="x", align_bytes=64)
             for g in range(PASSES):
                 cols = slice(B * PACK * g, B * PACK * (g + 1))
                 nc.vector.tensor_scalar_mul(out=x[:, cols], in0=cv_mx[:, cols], scalar1=adj_col[:, i, g : g + 1])
@@ -277,32 +277,35 @@ def tile_structuralequationmodels_e_kernel(
 
         def norm_variance(i):
             y = live["y", i]
+            first = i - i % PAIR
+            if i == first:
+                live["square_sum", first] = work.tile([P, PAIR * B_TILES], F32, name="square_sum", bufs=3)
+            square_sum = live["square_sum", first]
             minus_mean = work.tile([P, B_TILES], F32, name="minus_mean", bufs=3)
             squares = work.tile([P, V], BF16, name="squares")
-            square_sum = work.tile([P, B_TILES], F32, name="square_sum", bufs=3)
-            var_eps = work.tile([P, B_TILES], F32, name="var_eps", bufs=3)
-            rstd = work.tile([P, B_TILES], F32, name="rstd", bufs=5)
             nc.scalar.mul(out=minus_mean[:], in_=live["y_sum", i][:], mul=-1.0 / V)
             for bt in range(B_TILES):
+                col = B_TILES * (i - first) + bt
                 nc.scalar.activation(
                     out=squares[:],
                     in_=y[:, bt, :],
                     func=ACT.Square,
                     bias=minus_mean[:, bt : bt + 1],
                     scale=1.0,
-                    accum_out=square_sum[:, bt : bt + 1],
+                    accum_out=square_sum[:, col : col + 1],
                 )
-            nc.gpsimd.tensor_scalar(
-                out=var_eps[:], in0=square_sum[:], scalar1=1.0 / V, scalar2=LN_EPS, op0=ALU.mult, op1=ALU.add
-            )
-            nc.gpsimd.tensor_tensor(out=rstd[:], in0=var_eps[:], in1=minus_half[:], op=ALU.pow)
             live["minus_mean", i] = minus_mean
-            live["rstd", i] = rstd
+            if i == first + PAIR - 1:
+                var_eps = work.tile([P, PAIR * B_TILES], F32, name="var_eps", bufs=3)
+                rstd = work.tile([P, PAIR * B_TILES], F32, name="rstd", bufs=4)
+                nc.scalar.activation(out=var_eps[:], in_=square_sum[:], func=ACT.Identity, bias=eps_col[:], scale=1.0 / V)
+                nc.gpsimd.tensor_tensor(out=rstd[:], in0=var_eps[:], in1=minus_half[:], op=ALU.pow)
+                live["rstd", first] = rstd
 
         def norm_gain(i):
             y = live["y", i]
             minus_mean = live["minus_mean", i]
-            centred = work.tile([P, B_TILES, V], F32, name="centred", bufs=4)
+            centred = work.tile([P, B_TILES, V], F32, name="centred", bufs=5)
             for bt in range(B_TILES):
                 nc.vector.scalar_tensor_tensor(
                     out=centred[:, bt, :],
@@ -316,22 +319,22 @@ def tile_structuralequationmodels_e_kernel(
 
         def norm_shift_and_store(i):
             centred = live["centred", i]
-            rstd = live["rstd", i]
-            first = i - i % STORE_GROUP
+            first = i - i % PAIR
+            rstd = live["rstd", first]
             if i == first:
-                live["result", first] = work.tile([P, B_TILES, STORE_GROUP, V], F32, name="result", bufs=3)
+                live["result", first] = work.tile([P, B_TILES, PAIR, V], F32, name="result", bufs=3)
             result = live["result", first]
             for bt in range(B_TILES):
                 nc.vector.scalar_tensor_tensor(
                     out=result[:, bt, i - first, :],
                     in0=centred[:, bt, :],
-                    scalar=rstd[:, bt : bt + 1],
+                    scalar=rstd[:, B_TILES * (i - first) + bt : B_TILES * (i - first) + bt + 1],
                     in1=beta_rows[:, V * i : V * (i + 1)],
                     op0=ALU.mult,
                     op1=ALU.add,
                 )
-            if i == first + STORE_GROUP - 1:
-                nc.sync.dma_start(out=out_dram[:, :, first : first + STORE_GROUP, :], in_=result[:])
+            if i == first + PAIR - 1:
+                nc.sync.dma_start(out=out_dram[:, :, first : first + PAIR, :], in_=result[:])
 
         def run(stage, i):
             if 0 <= i < D:
@@ -340,8 +343,13 @@ def tile_structuralequationmodels_e_kernel(
         for i in range(2):
             scale_x(i)
             quantise_x(i)
-        for s in range(D + 9):
-            run(norm_shift_and_store, s - 8)
+
+        repeat_on_all_partitions(0, b2_rows, 6)
+        repeat_on_all_partitions(1, gamma_rows, 4)
+        repeat_on_all_partitions(2, beta_rows, 6)
+
+        for s in range(D + 10):
+            run(norm_shift_and_store, s - 9)
             run(load_equation, s + LOOKAHEAD)
             run(gelu, s - 1)
             run(norm_mean, s - 5)
@@ -353,6 +361,6 @@ def tile_structuralequationmodels_e_kernel(
             run(quantise_x, s + 2)
             run(quantise_h, s - 3)
             run(layer1, s)
-            run(words_of_h, s - 2)
             run(rows_of_h, s - 1)
+            run(words_of_h, s - 2)
             run(layer2, s - 3)

@@ -25,8 +25,10 @@ QUADRANTS = P // QUADRANT
 LIVE = 4
 BANK = 512
 LN_EPS = 1e-5
-PLANE_GROUP = 8
+PLANE_GROUP = 4
 LOOKAHEAD = 4
+W1_BUFS = 12
+PLANE_BUFS = 2
 PAIR = 2
 
 FLOPS = 2 * B * D * (K * H + H * V)
@@ -38,7 +40,7 @@ def tile_structuralequationmodels_e_kernel(
     nc = tc.nc
 
     w1_words_dram = W1_words.rearrange("g p n t -> g p (n t)").bitcast(I32).rearrange("g p n -> p g n")
-    w1_scales_dram = W1_scales.bitcast(I32).rearrange("(i g) q n -> g q i n", g=PASSES)
+    w1_scales_dram = W1_scales.bitcast(I32).rearrange("g q n -> q g n")
     w2_words_dram = W2_words.rearrange("i p v t -> i p (v t)").bitcast(I32).rearrange("i p v -> p i v")
     w2_scales_dram = W2_scales.bitcast(I32).rearrange("i q v -> q i v")
     cv_dram = causal_vars.rearrange("(c b) j v -> b c (j v)", b=P)
@@ -50,6 +52,8 @@ def tile_structuralequationmodels_e_kernel(
         work = ctx.enter_context(tc.tile_pool(name="work", bufs=2))
         psum = ctx.enter_context(tc.psum_pool(name="psum", bufs=1))
 
+        live = {}
+
         def bank(k, shape, dtype, name):
             return psum.tile(shape, dtype, name=name, tag="bank%d" % k)
 
@@ -60,8 +64,9 @@ def tile_structuralequationmodels_e_kernel(
         minus_half = keep.tile([P, PAIR * B_TILES], F32)
         eps_col = keep.tile([P, 1], F32)
         cv_mx = keep.tile([P, PASSES * B * PACK], BF16, align_bytes=64)
-        w1_words = [keep.tile([P, PASSES, H], I32, name="w1_words%d" % i, align_bytes=64) for i in range(D)]
-        w1_planes = keep.tile([P, D, H], U8, align_bytes=64)
+        w1_planes = [
+            keep.tile([P, PLANE_GROUP * PASSES, H], U8, name="w1_planes%d" % k, align_bytes=64) for k in range(PLANE_BUFS)
+        ]
         w2_words = keep.tile([P, D, V], I32, align_bytes=64)
         w2_planes = keep.tile([P, D, V], U8, align_bytes=64)
         b2_rows = keep.tile([P, D * V], BF16)
@@ -72,36 +77,35 @@ def tile_structuralequationmodels_e_kernel(
         select = keep.tile([P, QUADRANTS, P], BF16)
         b1_rows = keep.tile([P, P], BF16)
 
+        def load_planes(planes, scales_dram):
+            for r in range(LIVE):
+                nc.sync.dma_start(
+                    out=planes[r:P:QUADRANT, :, :].bitcast(I32), in_=scales_dram[r : QUADRANTS * LIVE : LIVE, :, :]
+                )
+
+        def planes_of(i):
+            return w1_planes[i // PLANE_GROUP % PLANE_BUFS]
+
         def load_equation(i):
             if i % PLANE_GROUP == 0:
-                group = slice(i, i + PLANE_GROUP)
-                for quadrant in range(QUADRANTS):
-                    for r in range(LIVE):
-                        first = QUADRANT * quadrant + r
-                        nc.sync.dma_start(
-                            out=w1_planes[first : first + LIVE * PASSES : LIVE, group, :].bitcast(I32),
-                            in_=w1_scales_dram[:, LIVE * quadrant + r, group, :],
-                        )
-            nc.sync.dma_start(out=w1_words[i][:], in_=w1_words_dram[:, PASSES * i : PASSES * (i + 1), :])
+                load_planes(planes_of(i), w1_scales_dram[:, PASSES * i : PASSES * (i + PLANE_GROUP), :])
+            w1_words = work.tile([P, PASSES, H], I32, name="w1_words", bufs=W1_BUFS, align_bytes=64)
+            nc.sync.dma_start(out=w1_words[:], in_=w1_words_dram[:, PASSES * i : PASSES * (i + 1), :])
             nc.sync.dma_start(out=w2_words[:, i, :], in_=w2_words_dram[:, i, :])
+            live["w1_words", i] = w1_words
 
-        for g in range(PASSES):
-            nc.sync.dma_start(out=cv_rows[:, g, :, :], in_=cv_dram[:, :, K_PASS * g : K_PASS * (g + 1)])
         nc.vector.memset(vectors[:], 0.0)
+        nc.vector.memset(b1_rows[:], 0.0)
+        for planes in (w1_planes[0], w2_planes):
+            nc.vector.memset(planes[:].bitcast(I32), 0)
         for r, vector in enumerate((b2, gamma, beta, adj_soft)):
             row = vector.rearrange("i v -> (i v)").unsqueeze(0)
             nc.scalar.dma_start(out=vectors[QUADRANT * r : QUADRANT * r + 1, 0 : row.shape[1]], in_=row)
-        nc.vector.memset(b1_rows[:], 0.0)
+        for g in range(PASSES):
+            nc.sync.dma_start(out=cv_rows[:, g, :, :], in_=cv_dram[:, :, K_PASS * g : K_PASS * (g + 1)])
         nc.scalar.dma_start(out=b1_rows[0 : D * H_TILES, :], in_=b1.rearrange("i (c m) -> (i c) m", m=P))
-        for i in range(0, D, PLANE_GROUP):
-            nc.vector.memset(w1_planes[:, i : i + PLANE_GROUP, :].bitcast(I32), 0)
-        nc.vector.memset(w2_planes[:].bitcast(I32), 0)
         load_equation(0)
-        for quadrant in range(QUADRANTS):
-            nc.sync.dma_start(
-                out=w2_planes[QUADRANT * quadrant : QUADRANT * quadrant + LIVE, :, :].bitcast(I32),
-                in_=w2_scales_dram[LIVE * quadrant : LIVE * (quadrant + 1), :, :],
-            )
+        load_planes(w2_planes, w2_scales_dram)
         for i in range(1, LOOKAHEAD):
             load_equation(i)
 
@@ -148,12 +152,6 @@ def tile_structuralequationmodels_e_kernel(
             rows = slice(QUADRANT * quadrant, QUADRANT * (quadrant + 1))
             nc.vector.tensor_copy(out=adj_col[rows, :, :], in_=adj_by_quadrant[rows, :, :, quadrant])
 
-        b1_psum = bank(5, [P, P], BF16, "b1_psum")
-        nc.tensor.transpose(b1_psum[:], b1_rows[:], ident_bf16[:])
-        nc.vector.tensor_copy(out=b1_col[:], in_=b1_psum[:, 0 : D * H_TILES])
-
-        live = {}
-
         def scale_x(i):
             x = work.tile([P, PASSES * B * PACK], BF16, name="x", tag="x", align_bytes=64)
             for g in range(PASSES):
@@ -179,8 +177,8 @@ def tile_structuralequationmodels_e_kernel(
                         b_cols = slice(B * g, B * (g + 1))
                         nc.tensor.matmul_mx(
                             out=h_psum[:, c2, :],
-                            lhsT=w1_words[i][:, g, n_cols].bitcast(FP8X4),
-                            lhsT_scale=w1_planes[LIVE * g : P, i, n_cols],
+                            lhsT=live["w1_words", i][:, g, n_cols].bitcast(FP8X4),
+                            lhsT_scale=planes_of(i)[:, PASSES * (i % PLANE_GROUP) + g, n_cols],
                             rhs=x_codes[:, b_cols].bitcast(FP8X4),
                             rhs_scale=x_plane[:, b_cols],
                             start=(g == 0),
@@ -340,11 +338,17 @@ def tile_structuralequationmodels_e_kernel(
             if 0 <= i < D:
                 stage(i)
 
-        for i in range(2):
-            scale_x(i)
-            quantise_x(i)
+        scale_x(0)
+        quantise_x(0)
+        for planes in w1_planes[1:]:
+            nc.vector.memset(planes[:].bitcast(I32), 0)
+        scale_x(1)
+        quantise_x(1)
 
         repeat_on_all_partitions(0, b2_rows, 6)
+        b1_psum = bank(5, [P, P], BF16, "b1_psum")
+        nc.tensor.transpose(b1_psum[:], b1_rows[:], ident_bf16[:])
+        nc.scalar.copy(out=b1_col[:], in_=b1_psum[:, 0 : D * H_TILES])
         repeat_on_all_partitions(1, gamma_rows, 4)
         repeat_on_all_partitions(2, beta_rows, 6)
 

@@ -22,13 +22,15 @@ B_TILES = B // P
 H_TILES = H // P
 QUADRANT = 32
 QUADRANTS = P // QUADRANT
+VECTORS = 3
 LIVE = 4
 BANK = 512
 LN_EPS = 1e-5
-PLANE_GROUP = 4
+W2_GROUP = 4
 LOOKAHEAD = 4
 W1_BUFS = 12
-PLANE_BUFS = 2
+GROUP = 4
+SEED = 1597463007.0
 PAIR = 2
 
 FLOPS = 2 * B * D * (K * H + H * V)
@@ -40,7 +42,7 @@ def tile_structuralequationmodels_e_kernel(
     nc = tc.nc
 
     w1_words_dram = W1_words.rearrange("g p n t -> g p (n t)").bitcast(I32).rearrange("g p n -> p g n")
-    w1_scales_dram = W1_scales.bitcast(I32).rearrange("g q n -> q g n")
+    w1_scales_dram = W1_scales.bitcast(I32).rearrange("(i g) q n -> i g q n", g=PASSES)
     w2_words_dram = W2_words.rearrange("i p v t -> i p (v t)").bitcast(I32).rearrange("i p v -> p i v")
     w2_scales_dram = W2_scales.bitcast(I32).rearrange("i q v -> q i v")
     cv_dram = causal_vars.rearrange("(c b) j v -> b c (j v)", b=P)
@@ -64,9 +66,7 @@ def tile_structuralequationmodels_e_kernel(
         minus_half = keep.tile([P, PAIR * B_TILES], F32)
         eps_col = keep.tile([P, 1], F32)
         cv_mx = keep.tile([P, PASSES * B * PACK], BF16, align_bytes=64)
-        w1_planes = [
-            keep.tile([P, PLANE_GROUP * PASSES, H], U8, name="w1_planes%d" % k, align_bytes=64) for k in range(PLANE_BUFS)
-        ]
+        w1_planes = keep.tile([P, D, H], U8, align_bytes=64)
         w2_words = keep.tile([P, D, V], I32, align_bytes=64)
         w2_planes = keep.tile([P, D, V], U8, align_bytes=64)
         b2_rows = keep.tile([P, D * V], BF16)
@@ -74,54 +74,82 @@ def tile_structuralequationmodels_e_kernel(
         beta_rows = keep.tile([P, D * V], BF16)
         cv_rows = work.tile([P, PASSES, B_TILES, K_PASS], BF16, name="cv_rows", tag="x", align_bytes=64)
         vectors = keep.tile([P, D * V], BF16)
-        select = keep.tile([P, QUADRANTS, P], BF16)
+        select = keep.tile([P, VECTORS, P], BF16)
+        ones = keep.tile([P, P], BF16)
+        adj_rows = keep.tile([P, D * D], BF16)
         b1_rows = keep.tile([P, P], BF16)
 
-        def load_planes(planes, scales_dram):
-            for r in range(LIVE):
+        def load_w1_planes(i):
+            for quadrant in range(QUADRANTS):
+                first = QUADRANT * quadrant
                 nc.sync.dma_start(
-                    out=planes[r:P:QUADRANT, :, :].bitcast(I32), in_=scales_dram[r : QUADRANTS * LIVE : LIVE, :, :]
+                    out=w1_planes[first : first + PASSES * LIVE, i, :].bitcast(I32),
+                    in_=w1_scales_dram[i, :, LIVE * quadrant : LIVE * (quadrant + 1), :],
                 )
 
-        def planes_of(i):
-            return w1_planes[i // PLANE_GROUP % PLANE_BUFS]
+        def load_w2_planes():
+            for r in range(LIVE):
+                nc.sync.dma_start(
+                    out=w2_planes[r:P:QUADRANT, :, :].bitcast(I32), in_=w2_scales_dram[r : QUADRANTS * LIVE : LIVE, :, :]
+                )
+
+        def load_w2_words(i):
+            if i % W2_GROUP == 0:
+                nc.sync.dma_start(out=w2_words[:, i : i + W2_GROUP, :], in_=w2_words_dram[:, i : i + W2_GROUP, :])
 
         def load_equation(i):
-            if i % PLANE_GROUP == 0:
-                load_planes(planes_of(i), w1_scales_dram[:, PASSES * i : PASSES * (i + PLANE_GROUP), :])
+            load_w1_planes(i)
             w1_words = work.tile([P, PASSES, H], I32, name="w1_words", bufs=W1_BUFS, align_bytes=64)
-            nc.sync.dma_start(out=w1_words[:], in_=w1_words_dram[:, PASSES * i : PASSES * (i + 1), :])
-            nc.sync.dma_start(out=w2_words[:, i, :], in_=w2_words_dram[:, i, :])
+            if i == 0:
+                for half in range(2):
+                    cols = slice(H // 2 * half, H // 2 * (half + 1))
+                    nc.sync.dma_start(out=w1_words[:, :, cols], in_=w1_words_dram[:, 0:PASSES, cols])
+            else:
+                nc.sync.dma_start(out=w1_words[:], in_=w1_words_dram[:, PASSES * i : PASSES * (i + 1), :])
             live["w1_words", i] = w1_words
 
-        nc.vector.memset(vectors[:], 0.0)
-        nc.vector.memset(b1_rows[:], 0.0)
-        for planes in (w1_planes[0], w2_planes):
-            nc.vector.memset(planes[:].bitcast(I32), 0)
-        for r, vector in enumerate((b2, gamma, beta, adj_soft)):
-            row = vector.rearrange("i v -> (i v)").unsqueeze(0)
-            nc.scalar.dma_start(out=vectors[QUADRANT * r : QUADRANT * r + 1, 0 : row.shape[1]], in_=row)
-        for g in range(PASSES):
-            nc.sync.dma_start(out=cv_rows[:, g, :, :], in_=cv_dram[:, :, K_PASS * g : K_PASS * (g + 1)])
-        nc.scalar.dma_start(out=b1_rows[0 : D * H_TILES, :], in_=b1.rearrange("i (c m) -> (i c) m", m=P))
-        load_equation(0)
-        load_planes(w2_planes, w2_scales_dram)
-        for i in range(1, LOOKAHEAD):
-            load_equation(i)
-
-        nc.vector.memset(select[:], 0.0)
-        for r in range(QUADRANTS):
-            nc.vector.memset(select[QUADRANT * r : QUADRANT * r + 1, r, :], 1.0)
         nc.vector.memset(minus_half[:], -0.5)
+        warm = keep.tile([P, 1], F32)
+        nc.scalar.activation(out=warm[:], in_=minus_half[:, 0:1], func=ACT.Gelu)
+        make_identity(nc, ident_f32[:])
+        nc.vector.memset(adj_rows[:].bitcast(I32), 0)
+        nc.vector.memset(ones[:], 1.0)
+        nc.vector.memset(w1_planes[:, 0:LOOKAHEAD, :].bitcast(I32), 0)
+        nc.vector.memset(b1_rows[:].bitcast(I32), 0)
+
+        def load_cv(g):
+            nc.sync.dma_start(out=cv_rows[:, g, :, :], in_=cv_dram[:, :, K_PASS * g : K_PASS * (g + 1)])
+
+        load_cv(0)
+        load_cv(1)
+        nc.sync.dma_start(out=adj_rows[0:1, :], in_=adj_soft.rearrange("i v -> (i v)").unsqueeze(0))
+        nc.scalar.dma_start(out=b1_rows[0 : D * H_TILES, :], in_=b1.rearrange("i (c m) -> (i c) m", m=P))
+        load_cv(2)
+        load_cv(3)
+        load_equation(0)
+        load_equation(1)
+        nc.vector.memset(vectors[:].bitcast(I32), 0)
+        make_identity(nc, ident_bf16[:])
+        nc.vector.memset(w2_planes[:].bitcast(I32), 0)
+        nc.vector.memset(w1_planes[:, LOOKAHEAD:, :].bitcast(I32), 0)
+        for r, vector in enumerate((b2, gamma, beta)):
+            row = vector.rearrange("i v -> (i v)").unsqueeze(0)
+            nc.sync.dma_start(out=vectors[QUADRANT * r : QUADRANT * r + 1, :], in_=row)
+        load_equation(2)
+        load_w2_planes()
+        load_w2_words(0)
+        load_equation(3)
+
+        nc.vector.memset(select[:].bitcast(I32), 0)
+        for r in range(VECTORS):
+            nc.vector.memset(select[QUADRANT * r : QUADRANT * r + 1, r, :], 1.0)
         nc.vector.tensor_scalar(
             out=eps_col[:], in0=minus_half[:, 0:1], scalar1=0.0, scalar2=LN_EPS, op0=ALU.mult, op1=ALU.add
         )
-        make_identity(nc, ident_f32[:])
-        make_identity(nc, ident_bf16[:])
 
-        def repeat_on_all_partitions(r, repeated, first_bank):
+        def repeat_on_all_partitions(r, repeated):
             for j in range(D * V // (2 * BANK)):
-                vector_psum = bank(first_bank + j, [P, 2 * BANK], BF16, "vector_psum")
+                vector_psum = bank(6 + j, [P, 2 * BANK], BF16, "vector_psum")
                 for half in range(2):
                     cols = slice(BANK * half, BANK * (half + 1))
                     nc.tensor.matmul(
@@ -133,177 +161,265 @@ def tile_structuralequationmodels_e_kernel(
                     )
                 nc.scalar.copy(out=repeated[:, 2 * BANK * j : 2 * BANK * (j + 1)], in_=vector_psum[:])
 
-        for g in range(PASSES):
+        def transpose_cv(g):
             cv_psum = bank(g, [P, 2, B_TILES, P], F32, "cv_psum")
             for c in range(B_TILES):
                 words = cv_rows[:, g, c, :].bitcast(F32)
                 for u in range(2):
                     nc.tensor.transpose(cv_psum[:, u, c, :], words[:, u : 2 * P : 2], ident_f32[:])
-            copy = nc.vector.tensor_copy if g % 2 == 0 else nc.scalar.copy
-            copy(
+            nc.scalar.copy(
                 out=cv_mx[:, B * PACK * g : B * PACK * (g + 1)].bitcast(F32).rearrange("p (b u) -> p b u", u=2),
                 in_=cv_psum[:].rearrange("p u c b -> p (c b) u"),
             )
 
+        transpose_cv(0)
         adj_psum = bank(4, [P, D * D], F32, "adj_psum")
-        nc.tensor.matmul(adj_psum[:], lhsT=select[:, 3, :], rhs=vectors[:, 0 : D * D], start=True, stop=True)
+        nc.tensor.matmul(adj_psum[:], lhsT=ones[:], rhs=adj_rows[:], start=True, stop=True)
         adj_by_quadrant = adj_psum[:].rearrange("p (i g q) -> p i g q", g=PASSES, q=QUADRANTS)
         for quadrant in range(QUADRANTS):
             rows = slice(QUADRANT * quadrant, QUADRANT * (quadrant + 1))
             nc.vector.tensor_copy(out=adj_col[rows, :, :], in_=adj_by_quadrant[rows, :, :, quadrant])
+        for g in range(1, PASSES):
+            transpose_cv(g)
+        b1_psum = bank(5, [P, P], BF16, "b1_psum")
+        nc.tensor.transpose(b1_psum[:], b1_rows[:], ident_bf16[:])
+        nc.scalar.copy(out=b1_col[:], in_=b1_psum[:, 0 : D * H_TILES])
+
+        small_steps = []
+
+        def one_small_step():
+            if small_steps:
+                small_steps.pop(0)()
+
+        def scale_pass(i, g):
+            if g == 0:
+                live["x", i] = work.tile([P, PASSES * B * PACK], BF16, name="x", tag="x", align_bytes=64)
+            cols = slice(B * PACK * g, B * PACK * (g + 1))
+            nc.vector.tensor_scalar_mul(
+                out=live["x", i][:, cols], in0=cv_mx[:, cols], scalar1=adj_col[:, i, g : g + 1]
+            )
+            one_small_step()
 
         def scale_x(i):
-            x = work.tile([P, PASSES * B * PACK], BF16, name="x", tag="x", align_bytes=64)
             for g in range(PASSES):
-                cols = slice(B * PACK * g, B * PACK * (g + 1))
-                nc.vector.tensor_scalar_mul(out=x[:, cols], in0=cv_mx[:, cols], scalar1=adj_col[:, i, g : g + 1])
-            live["x", i] = x
+                scale_pass(i, g)
+
+        def quantise_passes(i, first, last):
+            if first == 0:
+                live["x_codes", i] = work.tile([P, PASSES * B], U32, name="x_codes", bufs=3, align_bytes=64)
+                live["x_plane", i] = work.tile([P, PASSES * B], U8, name="x_plane", bufs=3, align_bytes=64)
+            nc.vector.quantize_mx(
+                out=live["x_codes", i][:, B * first : B * last].bitcast(FP8X4),
+                scales=live["x_plane", i][:, B * first : B * last],
+                in_=live["x", i][:, B * PACK * first : B * PACK * last],
+            )
+            one_small_step()
 
         def quantise_x(i):
-            x_codes = work.tile([P, PASSES * B], U32, name="x_codes", bufs=3, align_bytes=64)
-            x_plane = work.tile([P, PASSES * B], U8, name="x_plane", bufs=3, align_bytes=64)
-            nc.vector.quantize_mx(out=x_codes[:].bitcast(FP8X4), scales=x_plane[:], in_=live["x", i][:])
-            live["x_codes", i] = x_codes
-            live["x_plane", i] = x_plane
+            quantise_passes(i, 0, PASSES)
 
-        def layer1(i):
+        def layer1_half(i, half):
             x_codes = live["x_codes", i]
             x_plane = live["x_plane", i]
-            for half in range(2):
-                h_psum = bank(2 * (i % 2) + half, [P, 2, B], F32, "h_psum")
-                for c2 in range(2):
-                    n_cols = slice(P * (2 * half + c2), P * (2 * half + c2 + 1))
-                    for g in range(PASSES):
-                        b_cols = slice(B * g, B * (g + 1))
-                        nc.tensor.matmul_mx(
-                            out=h_psum[:, c2, :],
-                            lhsT=live["w1_words", i][:, g, n_cols].bitcast(FP8X4),
-                            lhsT_scale=planes_of(i)[:, PASSES * (i % PLANE_GROUP) + g, n_cols],
-                            rhs=x_codes[:, b_cols].bitcast(FP8X4),
-                            rhs_scale=x_plane[:, b_cols],
-                            start=(g == 0),
-                            stop=(g == PASSES - 1),
-                        )
-                live["h_psum", i, half] = h_psum
+            h_psum = bank(2 * (i % 2) + half, [P, 2, B], F32, "h_psum")
+            for c2 in range(2):
+                n_cols = slice(P * (2 * half + c2), P * (2 * half + c2 + 1))
+                for g in range(PASSES):
+                    b_cols = slice(B * g, B * (g + 1))
+                    nc.tensor.matmul_mx(
+                        out=h_psum[:, c2, :],
+                        lhsT=live["w1_words", i][:, g, n_cols].bitcast(FP8X4),
+                        lhsT_scale=w1_planes[LIVE * g :, i, n_cols],
+                        rhs=x_codes[:, b_cols].bitcast(FP8X4),
+                        rhs_scale=x_plane[:, b_cols],
+                        start=(g == 0),
+                        stop=(g == PASSES - 1),
+                    )
+            live["h_psum", i, half] = h_psum
 
-        def gelu(i):
-            h_cols = work.tile([P, H_TILES, B], BF16, name="h_cols")
-            for c in range(H_TILES):
+        def layer1(i):
+            layer1_half(i, 0)
+            layer1_half(i, 1)
+
+        def gelu_half(i, half):
+            if half == 0:
+                live["h_cols", i] = work.tile([P, H_TILES, B], BF16, name="h_cols")
+            for c in (2 * half, 2 * half + 1):
                 nc.scalar.activation(
-                    out=h_cols[:, c, :],
-                    in_=live["h_psum", i, c // 2][:, c % 2, :],
+                    out=live["h_cols", i][:, c, :],
+                    in_=live["h_psum", i, half][:, c % 2, :],
                     func=ACT.Gelu,
                     bias=b1_col[:, H_TILES * i + c : H_TILES * i + c + 1],
                     scale=1.0,
                 )
-            live["h_cols", i] = h_cols
 
-        def rows_of_h(i):
-            h_cols = live["h_cols", i]
-            h_rows_psum = bank(4, [P, B_TILES, H], BF16, "h_rows_psum")
-            for c in range(H_TILES):
-                for bt in range(B_TILES):
-                    nc.tensor.transpose(
-                        h_rows_psum[:, bt, P * c : P * (c + 1)], h_cols[:, c, P * bt : P * (bt + 1)], ident_bf16[:]
+        def gelu(i):
+            gelu_half(i, 0)
+            gelu_half(i, 1)
+
+        def rows_of_h(i, bts=(0, 1), k=4):
+            h_rows_psum = bank(k, [P, B_TILES, H], BF16, "h_rows_psum")
+            for bt in bts:
+                live["h_rows_psum", i, bt] = h_rows_psum
+                for c in range(H_TILES):
+                    nc.tensor.matmul(
+                        h_rows_psum[:, bt, P * c : P * (c + 1)],
+                        lhsT=live["h_cols", i][:, c, P * bt : P * (bt + 1)],
+                        rhs=ident_bf16[:],
+                        start=True,
+                        stop=True,
                     )
-            live["h_rows_psum", i] = h_rows_psum
 
-        def sort_words(i):
-            h_rows = work.tile([P, B_TILES, 2, P], F32, name="h_rows")
-            nc.scalar.copy(
-                out=h_rows[:],
-                in_=live["h_rows_psum", i][:].bitcast(F32).rearrange("b c (p u) -> b c u p", u=2),
+        def sort_words(i, bts=(0, 1), copy=nc.scalar.copy):
+            if bts[0] == 0:
+                live["h_rows", i] = work.tile([P, B_TILES, 2, P], F32, name="h_rows")
+            tiles = slice(bts[0], bts[-1] + 1)
+            copy(
+                out=live["h_rows", i][:, tiles, :, :],
+                in_=live["h_rows_psum", i, bts[0]][:, tiles, :].bitcast(F32).rearrange("b c (p u) -> b c u p", u=2),
             )
-            live["h_rows", i] = h_rows
 
-        def words_of_h(i):
-            h_rows = live["h_rows", i]
-            h_words_psum = bank(5, [P, 2, B_TILES, P], F32, "h_words_psum")
-            for u in range(2):
-                for bt in range(B_TILES):
-                    nc.tensor.transpose(h_words_psum[:, u, bt, :], h_rows[:, bt, u, :], ident_f32[:])
-            live["h_words_psum", i] = h_words_psum
+        def words_of_h(i, bts=(0, 1), k=5):
+            h_words_psum = bank(k, [P, 2, B_TILES, P], F32, "h_words_psum")
+            for bt in bts:
+                live["h_words_psum", i, bt] = h_words_psum
+                for u in range(2):
+                    nc.tensor.transpose(h_words_psum[:, u, bt, :], live["h_rows", i][:, bt, u, :], ident_f32[:])
 
-        def interleave(i):
-            h_mx = work.tile([P, B * PACK], BF16, name="h_mx", align_bytes=64)
-            nc.scalar.copy(
-                out=h_mx[:].bitcast(F32).rearrange("p (b u) -> p b u", u=2),
-                in_=live["h_words_psum", i][:].rearrange("p u c b -> p (c b) u"),
+        def interleave(i, bts=(0, 1), copy=nc.scalar.copy):
+            if bts[0] == 0:
+                live["h_mx", i] = work.tile([P, B * PACK], BF16, name="h_mx", align_bytes=64)
+            tiles = slice(bts[0], bts[-1] + 1)
+            cols = slice(P * PACK * bts[0], P * PACK * (bts[-1] + 1))
+            copy(
+                out=live["h_mx", i][:, cols].bitcast(F32).rearrange("p (b u) -> p b u", u=2),
+                in_=live["h_words_psum", i, bts[0]][:, :, tiles, :].rearrange("p u c b -> p (c b) u"),
             )
-            live["h_mx", i] = h_mx
 
-        def quantise_h(i):
-            h_codes = work.tile([P, B], U32, name="h_codes", align_bytes=64)
-            h_plane = work.tile([P, B], U8, name="h_plane", align_bytes=64)
-            nc.vector.quantize_mx(out=h_codes[:].bitcast(FP8X4), scales=h_plane[:], in_=live["h_mx", i][:])
-            live["h_codes", i] = h_codes
-            live["h_plane", i] = h_plane
+        def quantise_h(i, bts=(0, 1)):
+            if bts[0] == 0:
+                live["h_codes", i] = work.tile([P, B], U32, name="h_codes", bufs=3, align_bytes=64)
+                live["h_plane", i] = work.tile([P, B], U8, name="h_plane", bufs=3, align_bytes=64)
+            cols = slice(P * bts[0], P * (bts[-1] + 1))
+            nc.vector.quantize_mx(
+                out=live["h_codes", i][:, cols].bitcast(FP8X4),
+                scales=live["h_plane", i][:, cols],
+                in_=live["h_mx", i][:, PACK * P * bts[0] : PACK * P * (bts[-1] + 1)],
+            )
+            one_small_step()
 
-        def layer2(i):
-            h_codes = live["h_codes", i]
-            h_plane = live["h_plane", i]
-            y_psum = bank(6 + i % 2, [P, B_TILES, V], F32, "y_psum")
-            for bt in range(B_TILES):
+        def layer2(i, bts=(0, 1), k=None):
+            y_psum = bank(6 + i % 2 if k is None else k, [P, B_TILES, V], F32, "y_psum")
+            for bt in bts:
+                live["y_psum", i, bt] = y_psum
                 b_cols = slice(P * bt, P * (bt + 1))
                 nc.tensor.matmul_mx(
                     out=y_psum[:, bt, :],
-                    lhsT=h_codes[:, b_cols].bitcast(FP8X4),
-                    lhsT_scale=h_plane[:, b_cols],
+                    lhsT=live["h_codes", i][:, b_cols].bitcast(FP8X4),
+                    lhsT_scale=live["h_plane", i][:, b_cols],
                     rhs=w2_words[:, i, :].bitcast(FP8X4),
                     rhs_scale=w2_planes[:, i, :],
                     start=True,
                     stop=True,
                 )
-            live["y_psum", i] = y_psum
 
-        def norm_mean(i):
-            y_psum = live["y_psum", i]
-            y = work.tile([P, B_TILES, V], F32, name="y", bufs=3)
-            y_sum = work.tile([P, B_TILES], F32, name="y_sum", bufs=3)
-            for bt in range(B_TILES):
+        def norm_mean(i, bts=(0, 1)):
+            if bts[0] == 0:
+                live["y", i] = work.tile([P, B_TILES, V], F32, name="y", bufs=13)
+                live["y_sum", i] = work.tile([P, B_TILES], F32, name="y_sum", bufs=4)
+            for bt in bts:
                 nc.vector.scalar_tensor_tensor(
-                    out=y[:, bt, :],
-                    in0=y_psum[:, bt, :],
+                    out=live["y", i][:, bt, :],
+                    in0=live["y_psum", i, bt][:, bt, :],
                     scalar=1.0,
                     in1=b2_rows[:, V * i : V * (i + 1)],
                     op0=ALU.mult,
                     op1=ALU.add,
-                    accum_out=y_sum[:, bt : bt + 1],
+                    accum_out=live["y_sum", i][:, bt : bt + 1],
                 )
-            live["y", i] = y
-            live["y_sum", i] = y_sum
+                one_small_step()
 
-        def norm_variance(i):
-            y = live["y", i]
-            first = i - i % PAIR
-            if i == first:
-                live["square_sum", first] = work.tile([P, PAIR * B_TILES], F32, name="square_sum", bufs=3)
+        def group_of(i):
+            return (i - i % GROUP, GROUP) if i < D - GROUP else (i - i % PAIR, PAIR)
+
+        def norm_variance(i, bts=(0, 1)):
+            first, size = group_of(i)
+            if i == first and bts[0] == 0:
+                live["square_sum", first] = work.tile([P, GROUP * B_TILES], F32, name="square_sum", bufs=4)
+            if bts[0] == 0:
+                live["minus_mean", i] = work.tile([P, B_TILES], F32, name="minus_mean", bufs=13)
             square_sum = live["square_sum", first]
-            minus_mean = work.tile([P, B_TILES], F32, name="minus_mean", bufs=3)
+            minus_mean = live["minus_mean", i]
             squares = work.tile([P, V], BF16, name="squares")
-            nc.scalar.mul(out=minus_mean[:], in_=live["y_sum", i][:], mul=-1.0 / V)
-            for bt in range(B_TILES):
+            tiles = slice(bts[0], bts[-1] + 1)
+            nc.scalar.mul(out=minus_mean[:, tiles], in_=live["y_sum", i][:, tiles], mul=-1.0 / V)
+            for bt in bts:
                 col = B_TILES * (i - first) + bt
                 nc.scalar.activation(
                     out=squares[:],
-                    in_=y[:, bt, :],
+                    in_=live["y", i][:, bt, :],
                     func=ACT.Square,
                     bias=minus_mean[:, bt : bt + 1],
                     scale=1.0,
                     accum_out=square_sum[:, col : col + 1],
                 )
-            live["minus_mean", i] = minus_mean
-            if i == first + PAIR - 1:
-                var_eps = work.tile([P, PAIR * B_TILES], F32, name="var_eps", bufs=3)
-                rstd = work.tile([P, PAIR * B_TILES], F32, name="rstd", bufs=4)
-                nc.scalar.activation(out=var_eps[:], in_=square_sum[:], func=ACT.Identity, bias=eps_col[:], scale=1.0 / V)
-                nc.gpsimd.tensor_tensor(out=rstd[:], in0=var_eps[:], in1=minus_half[:], op=ALU.pow)
-                live["rstd", first] = rstd
+            if i == first + size - 1 and i < D - GROUP:
+                n = B_TILES * size
+                var_eps = work.tile([P, GROUP * B_TILES], F32, name="var_eps", bufs=4)
+                nc.scalar.activation(
+                    out=var_eps[:, 0:n], in_=square_sum[:, 0:n], func=ACT.Identity, bias=eps_col[:], scale=1.0 / V
+                )
+                live["var_eps", first] = var_eps
+
+        def norm_rstd_sqrt(i):
+            first, size = group_of(i)
+            n = B_TILES * size
+            std = work.tile([P, GROUP * B_TILES], F32, name="std")
+            nc.scalar.activation(
+                out=std[:, 0:n], in_=live["square_sum", first][:, 0:n], func=ACT.Sqrt, bias=eps_col[:], scale=1.0 / V
+            )
+            live["std", first] = std
+
+        def norm_rstd_reciprocal(i):
+            first, size = group_of(i)
+            n = B_TILES * size
+            std = live["std", first]
+            rstd = work.tile([P, GROUP * B_TILES], F32, name="rstd")
+            nc.vector.reciprocal(out=rstd[:, 0:n], in_=std[:, 0:n])
+            live["rstd", first] = rstd[:, 0:n]
+
+        def norm_rstd(i):
+            first, size = group_of(i)
+            if i != first + size - 1:
+                return
+            a = live["var_eps", first]
+            bits = work.tile([P, GROUP * B_TILES], I32, name="bits")
+            small_steps.append(
+                lambda: nc.vector.tensor_scalar(
+                    out=bits[:], in0=a[:].bitcast(I32), scalar1=-0.5, scalar2=SEED, op0=ALU.mult, op1=ALU.add
+                )
+            )
+            r = bits[:].bitcast(F32)
+            for k in range(3):
+                square = work.tile([P, GROUP * B_TILES], F32, name="square%d" % k)
+                slope = work.tile([P, GROUP * B_TILES], F32, name="slope%d" % k)
+                better = work.tile([P, GROUP * B_TILES], F32, name="better%d" % k)
+                small_steps.extend(newton_step(a[:], r, square[:], slope[:], better[:]))
+                r = better[:]
+            live["rstd", first] = r
+
+        def newton_step(a, r, square, slope, better):
+            stt = nc.vector.scalar_tensor_tensor
+            return [
+                lambda: nc.vector.tensor_tensor(out=square, in0=r, in1=r, op=ALU.mult),
+                lambda: stt(out=slope, in0=square, scalar=-0.5, in1=a, op0=ALU.mult, op1=ALU.mult),
+                lambda: stt(out=better, in0=slope, scalar=1.5, in1=r, op0=ALU.add, op1=ALU.mult),
+            ]
 
         def norm_gain(i):
             y = live["y", i]
             minus_mean = live["minus_mean", i]
-            centred = work.tile([P, B_TILES, V], F32, name="centred", bufs=5)
+            centred = work.tile([P, B_TILES, V], F32, name="centred", bufs=9)
             for bt in range(B_TILES):
                 nc.vector.scalar_tensor_tensor(
                     out=centred[:, bt, :],
@@ -313,12 +429,14 @@ def tile_structuralequationmodels_e_kernel(
                     op0=ALU.add,
                     op1=ALU.mult,
                 )
+                one_small_step()
             live["centred", i] = centred
 
         def norm_shift_and_store(i):
             centred = live["centred", i]
             first = i - i % PAIR
-            rstd = live["rstd", first]
+            group_first = group_of(i)[0]
+            rstd = live["rstd", group_first]
             if i == first:
                 live["result", first] = work.tile([P, B_TILES, PAIR, V], F32, name="result", bufs=3)
             result = live["result", first]
@@ -326,11 +444,12 @@ def tile_structuralequationmodels_e_kernel(
                 nc.vector.scalar_tensor_tensor(
                     out=result[:, bt, i - first, :],
                     in0=centred[:, bt, :],
-                    scalar=rstd[:, B_TILES * (i - first) + bt : B_TILES * (i - first) + bt + 1],
+                    scalar=rstd[:, B_TILES * (i - group_first) + bt : B_TILES * (i - group_first) + bt + 1],
                     in1=beta_rows[:, V * i : V * (i + 1)],
                     op0=ALU.mult,
                     op1=ALU.add,
                 )
+                one_small_step()
             if i == first + PAIR - 1:
                 nc.sync.dma_start(out=out_dram[:, :, first : first + PAIR, :], in_=result[:])
 
@@ -338,33 +457,151 @@ def tile_structuralequationmodels_e_kernel(
             if 0 <= i < D:
                 stage(i)
 
-        scale_x(0)
-        quantise_x(0)
-        for planes in w1_planes[1:]:
-            nc.vector.memset(planes[:].bitcast(I32), 0)
+        def layer1_first(i):
+            layer1_half(i, 0)
+
+        def layer1_second(i):
+            layer1_half(i, 1)
+
+        def gelu_first(i):
+            gelu_half(i, 0)
+
+        def gelu_second(i):
+            gelu_half(i, 1)
+
+        def flush(i):
+            while small_steps:
+                one_small_step()
+
+        scale_pass(0, 0)
+        for g in range(1, PASSES):
+            scale_pass(0, g)
+            quantise_passes(0, g - 1, g)
+        quantise_passes(0, PASSES - 1, PASSES)
         scale_x(1)
         quantise_x(1)
 
-        repeat_on_all_partitions(0, b2_rows, 6)
-        b1_psum = bank(5, [P, P], BF16, "b1_psum")
-        nc.tensor.transpose(b1_psum[:], b1_rows[:], ident_bf16[:])
-        nc.scalar.copy(out=b1_col[:], in_=b1_psum[:, 0 : D * H_TILES])
-        repeat_on_all_partitions(1, gamma_rows, 4)
-        repeat_on_all_partitions(2, beta_rows, 6)
+        repeated = (b2_rows, gamma_rows, beta_rows)
 
-        for s in range(D + 10):
-            run(norm_shift_and_store, s - 9)
+        def rest_of_norm():
+            for j in range(D + LAG):
+                if j < D:
+                    rest.append((norm_gain, j))
+                if j >= LAG:
+                    rest.append((norm_shift_and_store, j - LAG))
+
+        LAG = 4
+        rest = []
+        rest_of_norm()
+
+        def ready(stage, j):
+            if stage is norm_gain:
+                return ("minus_mean", j) in live
+            return ("rstd", group_of(j)[0]) in live and not small_steps
+
+        def fill(n):
+            for k in range(n):
+                if rest and ready(*rest[0]):
+                    stage, j = rest.pop(0)
+                    stage(j)
+
+        for s in range(D - 2):
             run(load_equation, s + LOOKAHEAD)
+            run(load_w2_words, s + LOOKAHEAD)
+            run(norm_rstd, s - 7)
+            run(norm_mean, s - 6)
             run(gelu, s - 1)
-            run(norm_mean, s - 5)
             run(sort_words, s - 2)
             run(scale_x, s + 2)
             run(interleave, s - 3)
-            run(norm_gain, s - 6)
-            run(norm_variance, s - 5)
+            run(quantise_h, s - 4)
+            run(norm_variance, s - 6)
+            if s >= 7:
+                fill(1)
             run(quantise_x, s + 2)
-            run(quantise_h, s - 3)
+            flush(0)
+            if 1 <= s <= VECTORS:
+                repeat_on_all_partitions(s - 1, repeated[s - 1])
             run(layer1, s)
             run(rows_of_h, s - 1)
             run(words_of_h, s - 2)
-            run(layer2, s - 3)
+            run(layer2, s - 4)
+
+        last = D - 1
+        gelu(13)
+        sort_words(12)
+        interleave(11)
+        norm_rstd(7)
+        norm_mean(8)
+        quantise_h(10)
+        norm_variance(8)
+        fill(2)
+        quantise_h(11)
+        layer1(14)
+        rows_of_h(13)
+        words_of_h(12)
+        layer2(10)
+        gelu(14)
+        sort_words(13)
+        interleave(12)
+        norm_mean(9)
+        fill(3)
+        flush(0)
+        quantise_h(12)
+        layer1_half(last, 0)
+        rows_of_h(14)
+        words_of_h(13)
+        layer2(11)
+        gelu_half(last, 0)
+        sort_words(14)
+        interleave(13)
+        norm_mean(10)
+        fill(2)
+        norm_variance(9)
+        norm_variance(10)
+        quantise_h(13)
+        norm_mean(11)
+        fill(1)
+        layer1_half(last, 1)
+        words_of_h(14)
+        layer2(12)
+        layer2(13)
+        gelu_half(last, 1)
+        interleave(14)
+        fill(2)
+        rows_of_h(last, (0,), 0)
+        rows_of_h(last, (1,), 4)
+        norm_mean(12)
+        quantise_h(14)
+        sort_words(last, (0,))
+        sort_words(last, (1,), nc.vector.tensor_copy)
+        words_of_h(last, (0,), 1)
+        words_of_h(last, (1,), 5)
+        layer2(14)
+        norm_variance(11)
+        norm_rstd(11)
+        interleave(last, (0,))
+        norm_mean(13)
+        interleave(last, (1,), nc.vector.tensor_copy)
+        quantise_h(last, (0,))
+        quantise_h(last, (1,))
+        layer2(last, (0,), 0)
+        layer2(last, (1,), 4)
+        norm_variance(12)
+        norm_variance(13)
+        norm_mean(14)
+        fill(2)
+        norm_mean(last, (0,))
+        norm_mean(last, (1,))
+        norm_rstd_sqrt(13)
+        norm_variance(14)
+        norm_variance(last, (0,))
+        norm_variance(last, (1,))
+        norm_rstd_sqrt(last)
+        fill(2)
+        flush(0)
+        fill(4)
+        norm_rstd_reciprocal(13)
+        fill(4)
+        norm_rstd_reciprocal(last)
+        fill(2 * D)

@@ -22,7 +22,6 @@ B_TILES = B // P
 H_TILES = H // P
 QUADRANT = 32
 QUADRANTS = P // QUADRANT
-VECTORS = 3
 LIVE = 4
 BANK = 512
 LN_EPS = 1e-5
@@ -73,8 +72,9 @@ def tile_structuralequationmodels_e_kernel(
         gamma_rows = keep.tile([P, D * V], BF16)
         beta_rows = keep.tile([P, D * V], BF16)
         cv_rows = work.tile([P, PASSES, B_TILES, K_PASS], BF16, name="cv_rows", tag="x", align_bytes=64)
-        vectors = keep.tile([P, D * V], BF16)
-        select = keep.tile([P, VECTORS, P], BF16)
+        b2_row = keep.tile([P, D * V], BF16)
+        gain_rows = keep.tile([P, D * V], BF16)
+        select = keep.tile([P, 2, P], BF16)
         ones = keep.tile([P, P], BF16)
         adj_rows = keep.tile([P, D * D], BF16)
         b1_rows = keep.tile([P, P], BF16)
@@ -108,58 +108,56 @@ def tile_structuralequationmodels_e_kernel(
                 nc.sync.dma_start(out=w1_words[:], in_=w1_words_dram[:, PASSES * i : PASSES * (i + 1), :])
             live["w1_words", i] = w1_words
 
+        def load_cv(g):
+            nc.sync.dma_start(out=cv_rows[:, g, :, :], in_=cv_dram[:, :, K_PASS * g : K_PASS * (g + 1)])
+
+        def row_of(vector):
+            return vector.rearrange("i v -> (i v)").unsqueeze(0)
+
+        load_cv(0)
+        load_cv(1)
+        nc.vector.memset(adj_rows[:].bitcast(I32), 0)
+        nc.sync.dma_start(out=adj_rows[0:1, :], in_=row_of(adj_soft))
+        nc.vector.memset(b2_row[:].bitcast(I32), 0)
+        nc.scalar.dma_start(out=b2_row[0:1, :], in_=row_of(b2))
+        nc.vector.memset(b1_rows[:].bitcast(I32), 0)
+        nc.scalar.dma_start(out=b1_rows[0 : D * H_TILES, :], in_=b1.rearrange("i (c m) -> (i c) m", m=P))
+        load_cv(2)
+        load_cv(3)
         nc.vector.memset(minus_half[:], -0.5)
         warm = keep.tile([P, 1], F32)
         nc.scalar.activation(out=warm[:], in_=minus_half[:, 0:1], func=ACT.Gelu)
         make_identity(nc, ident_f32[:])
-        nc.vector.memset(adj_rows[:].bitcast(I32), 0)
-        nc.vector.memset(ones[:], 1.0)
+        make_identity(nc, ident_bf16[:])
         nc.vector.memset(w1_planes[:, 0:LOOKAHEAD, :].bitcast(I32), 0)
-        nc.vector.memset(b1_rows[:].bitcast(I32), 0)
-
-        def load_cv(g):
-            nc.sync.dma_start(out=cv_rows[:, g, :, :], in_=cv_dram[:, :, K_PASS * g : K_PASS * (g + 1)])
-
-        load_cv(0)
-        load_cv(1)
-        nc.sync.dma_start(out=adj_rows[0:1, :], in_=adj_soft.rearrange("i v -> (i v)").unsqueeze(0))
-        nc.scalar.dma_start(out=b1_rows[0 : D * H_TILES, :], in_=b1.rearrange("i (c m) -> (i c) m", m=P))
-        load_cv(2)
-        load_cv(3)
+        nc.vector.memset(ones[:], 1.0)
+        nc.vector.memset(gain_rows[:].bitcast(I32), 0)
+        nc.gpsimd.dma_start(out=gain_rows[0:1, :], in_=row_of(gamma))
+        nc.gpsimd.dma_start(out=gain_rows[QUADRANT : QUADRANT + 1, :], in_=row_of(beta))
         load_equation(0)
         load_equation(1)
-        nc.vector.memset(vectors[:].bitcast(I32), 0)
-        make_identity(nc, ident_bf16[:])
-        nc.vector.memset(w2_planes[:].bitcast(I32), 0)
-        nc.vector.memset(w1_planes[:, LOOKAHEAD:, :].bitcast(I32), 0)
-        for r, vector in enumerate((b2, gamma, beta)):
-            row = vector.rearrange("i v -> (i v)").unsqueeze(0)
-            nc.sync.dma_start(out=vectors[QUADRANT * r : QUADRANT * r + 1, :], in_=row)
         load_equation(2)
-        load_w2_planes()
-        load_w2_words(0)
         load_equation(3)
 
         nc.vector.memset(select[:].bitcast(I32), 0)
-        for r in range(VECTORS):
+        for r in range(2):
             nc.vector.memset(select[QUADRANT * r : QUADRANT * r + 1, r, :], 1.0)
         nc.vector.tensor_scalar(
             out=eps_col[:], in0=minus_half[:, 0:1], scalar1=0.0, scalar2=LN_EPS, op0=ALU.mult, op1=ALU.add
         )
 
-        def repeat_on_all_partitions(r, repeated):
+        def repeat_row(rows, pick, repeated):
             for j in range(D * V // (2 * BANK)):
-                vector_psum = bank(6 + j, [P, 2 * BANK], BF16, "vector_psum")
+                row_psum = bank(6 + j, [P, 2 * BANK], BF16, "row_psum")
                 for half in range(2):
-                    cols = slice(BANK * half, BANK * (half + 1))
                     nc.tensor.matmul(
-                        vector_psum[:, cols],
-                        lhsT=select[:, r, :],
-                        rhs=vectors[:, 2 * BANK * j + BANK * half : 2 * BANK * j + BANK * (half + 1)],
+                        row_psum[:, BANK * half : BANK * (half + 1)],
+                        lhsT=pick,
+                        rhs=rows[:, 2 * BANK * j + BANK * half : 2 * BANK * j + BANK * (half + 1)],
                         start=True,
                         stop=True,
                     )
-                nc.scalar.copy(out=repeated[:, 2 * BANK * j : 2 * BANK * (j + 1)], in_=vector_psum[:])
+                nc.scalar.copy(out=repeated[:, 2 * BANK * j : 2 * BANK * (j + 1)], in_=row_psum[:])
 
         def transpose_cv(g):
             cv_psum = bank(g, [P, 2, B_TILES, P], F32, "cv_psum")
@@ -181,6 +179,7 @@ def tile_structuralequationmodels_e_kernel(
             nc.vector.tensor_copy(out=adj_col[rows, :, :], in_=adj_by_quadrant[rows, :, :, quadrant])
         for g in range(1, PASSES):
             transpose_cv(g)
+        repeat_row(b2_row, ones[:], b2_rows)
         b1_psum = bank(5, [P, P], BF16, "b1_psum")
         nc.tensor.transpose(b1_psum[:], b1_rows[:], ident_bf16[:])
         nc.scalar.copy(out=b1_col[:], in_=b1_psum[:, 0 : D * H_TILES])
@@ -326,7 +325,8 @@ def tile_structuralequationmodels_e_kernel(
         def norm_mean(i, bts=(0, 1)):
             if bts[0] == 0:
                 live["y", i] = work.tile([P, B_TILES, V], F32, name="y", bufs=13)
-                live["y_sum", i] = work.tile([P, B_TILES], F32, name="y_sum", bufs=4)
+                if i % PAIR == 0:
+                    live["y_sum", i] = work.tile([P, PAIR * B_TILES], F32, name="y_sum", bufs=8)
             for bt in bts:
                 nc.vector.scalar_tensor_tensor(
                     out=live["y", i][:, bt, :],
@@ -335,7 +335,7 @@ def tile_structuralequationmodels_e_kernel(
                     in1=b2_rows[:, V * i : V * (i + 1)],
                     op0=ALU.mult,
                     op1=ALU.add,
-                    accum_out=live["y_sum", i][:, bt : bt + 1],
+                    accum_out=live["y_sum", i - i % PAIR][:, B_TILES * (i % PAIR) + bt : B_TILES * (i % PAIR) + bt + 1],
                 )
                 one_small_step()
 
@@ -346,28 +346,34 @@ def tile_structuralequationmodels_e_kernel(
             first, size = group_of(i)
             if i == first and bts[0] == 0:
                 live["square_sum", first] = work.tile([P, GROUP * B_TILES], F32, name="square_sum", bufs=4)
-            if bts[0] == 0:
-                live["minus_mean", i] = work.tile([P, B_TILES], F32, name="minus_mean", bufs=13)
             square_sum = live["square_sum", first]
-            minus_mean = live["minus_mean", i]
-            squares = work.tile([P, V], BF16, name="squares")
-            tiles = slice(bts[0], bts[-1] + 1)
-            nc.scalar.mul(out=minus_mean[:, tiles], in_=live["y_sum", i][:, tiles], mul=-1.0 / V)
+            y_sum = live["y_sum", i - i % PAIR]
             for bt in bts:
+                squares = work.tile([P, V], BF16, name="squares", bufs=4)
                 col = B_TILES * (i - first) + bt
+                pair_col = B_TILES * (i % PAIR) + bt
                 nc.scalar.activation(
                     out=squares[:],
                     in_=live["y", i][:, bt, :],
                     func=ACT.Square,
-                    bias=minus_mean[:, bt : bt + 1],
-                    scale=1.0,
+                    bias=y_sum[:, pair_col : pair_col + 1],
+                    scale=-float(V),
                     accum_out=square_sum[:, col : col + 1],
                 )
+            if i % PAIR == PAIR - 1 and bts[-1] == B_TILES - 1:
+                minus_mean = work.tile([P, PAIR * B_TILES], F32, name="minus_mean", bufs=8)
+                nc.scalar.mul(out=minus_mean[:], in_=y_sum[:], mul=-1.0 / V)
+                live["minus_mean", i - 1] = minus_mean[:, 0:B_TILES]
+                live["minus_mean", i] = minus_mean[:, B_TILES:]
             if i == first + size - 1 and i < D - GROUP:
                 n = B_TILES * size
                 var_eps = work.tile([P, GROUP * B_TILES], F32, name="var_eps", bufs=4)
                 nc.scalar.activation(
-                    out=var_eps[:, 0:n], in_=square_sum[:, 0:n], func=ACT.Identity, bias=eps_col[:], scale=1.0 / V
+                    out=var_eps[:, 0:n],
+                    in_=square_sum[:, 0:n],
+                    func=ACT.Identity,
+                    bias=eps_col[:],
+                    scale=1.0 / V**3,
                 )
                 live["var_eps", first] = var_eps
 
@@ -376,7 +382,7 @@ def tile_structuralequationmodels_e_kernel(
             n = B_TILES * size
             std = work.tile([P, GROUP * B_TILES], F32, name="std")
             nc.scalar.activation(
-                out=std[:, 0:n], in_=live["square_sum", first][:, 0:n], func=ACT.Sqrt, bias=eps_col[:], scale=1.0 / V
+                out=std[:, 0:n], in_=live["square_sum", first][:, 0:n], func=ACT.Sqrt, bias=eps_col[:], scale=1.0 / V**3
             )
             live["std", first] = std
 
@@ -438,7 +444,7 @@ def tile_structuralequationmodels_e_kernel(
             group_first = group_of(i)[0]
             rstd = live["rstd", group_first]
             if i == first:
-                live["result", first] = work.tile([P, B_TILES, PAIR, V], F32, name="result", bufs=3)
+                live["result", first] = work.tile([P, B_TILES, PAIR, V], F32, name="result", bufs=8)
             result = live["result", first]
             for bt in range(B_TILES):
                 nc.vector.scalar_tensor_tensor(
@@ -480,8 +486,12 @@ def tile_structuralequationmodels_e_kernel(
         quantise_passes(0, PASSES - 1, PASSES)
         scale_x(1)
         quantise_x(1)
+        nc.vector.memset(w2_planes[:].bitcast(I32), 0)
+        load_w2_planes()
+        load_w2_words(0)
+        nc.vector.memset(w1_planes[:, LOOKAHEAD:, :].bitcast(I32), 0)
 
-        repeated = (b2_rows, gamma_rows, beta_rows)
+        repeats = {1: (gain_rows, select[:, 0, :], gamma_rows), 2: (gain_rows, select[:, 1, :], beta_rows)}
 
         def rest_of_norm():
             for j in range(D + LAG):
@@ -516,26 +526,28 @@ def tile_structuralequationmodels_e_kernel(
             run(interleave, s - 3)
             run(quantise_h, s - 4)
             run(norm_variance, s - 6)
-            if s >= 7:
+            if s >= 8:
                 fill(1)
             run(quantise_x, s + 2)
             flush(0)
-            if 1 <= s <= VECTORS:
-                repeat_on_all_partitions(s - 1, repeated[s - 1])
+            if s in repeats:
+                repeat_row(*repeats[s])
             run(layer1, s)
             run(rows_of_h, s - 1)
             run(words_of_h, s - 2)
             run(layer2, s - 4)
 
+
         last = D - 1
+        norm_rstd(7)
         gelu(13)
         sort_words(12)
         interleave(11)
-        norm_rstd(7)
         norm_mean(8)
         quantise_h(10)
         norm_variance(8)
         fill(2)
+        flush(0)
         quantise_h(11)
         layer1(14)
         rows_of_h(13)
@@ -546,7 +558,6 @@ def tile_structuralequationmodels_e_kernel(
         interleave(12)
         norm_mean(9)
         fill(3)
-        flush(0)
         quantise_h(12)
         layer1_half(last, 0)
         rows_of_h(14)
@@ -556,12 +567,12 @@ def tile_structuralequationmodels_e_kernel(
         sort_words(14)
         interleave(13)
         norm_mean(10)
-        fill(2)
+        fill(3)
         norm_variance(9)
         norm_variance(10)
         quantise_h(13)
         norm_mean(11)
-        fill(1)
+        fill(3)
         layer1_half(last, 1)
         words_of_h(14)
         layer2(12)
@@ -572,6 +583,7 @@ def tile_structuralequationmodels_e_kernel(
         rows_of_h(last, (0,), 0)
         rows_of_h(last, (1,), 4)
         norm_mean(12)
+        fill(1)
         quantise_h(14)
         sort_words(last, (0,))
         sort_words(last, (1,), nc.vector.tensor_copy)
@@ -580,8 +592,8 @@ def tile_structuralequationmodels_e_kernel(
         layer2(14)
         norm_variance(11)
         norm_rstd(11)
-        interleave(last, (0,))
         norm_mean(13)
+        interleave(last, (0,))
         interleave(last, (1,), nc.vector.tensor_copy)
         quantise_h(last, (0,))
         quantise_h(last, (1,))
@@ -602,6 +614,6 @@ def tile_structuralequationmodels_e_kernel(
         flush(0)
         fill(4)
         norm_rstd_reciprocal(13)
-        fill(4)
+        fill(3)
         norm_rstd_reciprocal(last)
         fill(2 * D)

@@ -27,7 +27,7 @@ BANK = 512
 LN_EPS = 1e-5
 W2_GROUP = 4
 LOOKAHEAD = 4
-W1_BUFS = 12
+W1_BUFS = 10
 GROUP = 4
 SEED = 1597463007.0
 PAIR = 2
@@ -71,7 +71,7 @@ def tile_structuralequationmodels_e_kernel(
         b2_rows = keep.tile([P, D * V], BF16)
         gamma_rows = keep.tile([P, D * V], BF16)
         beta_rows = keep.tile([P, D * V], BF16)
-        cv_rows = work.tile([P, PASSES, B_TILES, K_PASS], BF16, name="cv_rows", tag="x", align_bytes=64)
+        cv_rows = work.tile([P, PASSES, B_TILES, K_PASS], BF16, name="cv_rows", tag="x", bufs=3, align_bytes=64)
         b2_row = keep.tile([P, D * V], BF16)
         gain_rows = keep.tile([P, D * V], BF16)
         select = keep.tile([P, 2, P], BF16)
@@ -192,16 +192,16 @@ def tile_structuralequationmodels_e_kernel(
 
         def scale_pass(i, g):
             if g == 0:
-                live["x", i] = work.tile([P, PASSES * B * PACK], BF16, name="x", tag="x", align_bytes=64)
+                live["x", i] = work.tile([P, PASSES * B * PACK], BF16, name="x", tag="x", bufs=3, align_bytes=64)
             cols = slice(B * PACK * g, B * PACK * (g + 1))
             nc.vector.tensor_scalar_mul(
                 out=live["x", i][:, cols], in0=cv_mx[:, cols], scalar1=adj_col[:, i, g : g + 1]
             )
             one_small_step()
 
-        def scale_x(i):
-            for g in range(PASSES):
-                scale_pass(i, g)
+        def next_pass(k):
+            if k < D * PASSES:
+                scale_pass(k // PASSES, k % PASSES)
 
         def quantise_passes(i, first, last):
             if first == 0:
@@ -340,7 +340,7 @@ def tile_structuralequationmodels_e_kernel(
                 one_small_step()
 
         def group_of(i):
-            return (i - i % GROUP, GROUP) if i < D - GROUP else (i - i % PAIR, PAIR)
+            return (i - i % GROUP, GROUP)
 
         def norm_variance(i, bts=(0, 1)):
             first, size = group_of(i)
@@ -484,7 +484,9 @@ def tile_structuralequationmodels_e_kernel(
             scale_pass(0, g)
             quantise_passes(0, g - 1, g)
         quantise_passes(0, PASSES - 1, PASSES)
-        scale_x(1)
+        next_pass(PASSES)
+        for g in range(1, PASSES + 1):
+            next_pass(PASSES + g)
         quantise_x(1)
         nc.vector.memset(w2_planes[:].bitcast(I32), 0)
         load_w2_planes()
@@ -510,22 +512,23 @@ def tile_structuralequationmodels_e_kernel(
             return ("rstd", group_of(j)[0]) in live and not small_steps
 
         def fill(n):
-            for k in range(n):
-                if rest and ready(*rest[0]):
-                    stage, j = rest.pop(0)
-                    stage(j)
+            for stage, j in [item for item in rest if ready(*item)][:n]:
+                rest.remove((stage, j))
+                stage(j)
 
         for s in range(D - 2):
             run(load_equation, s + LOOKAHEAD)
             run(load_w2_words, s + LOOKAHEAD)
             run(norm_rstd, s - 7)
-            run(norm_mean, s - 6)
-            run(gelu, s - 1)
-            run(sort_words, s - 2)
-            run(scale_x, s + 2)
-            run(interleave, s - 3)
-            run(quantise_h, s - 4)
+            run(norm_mean, s - 5)
+            run(gelu_first, s - 1)
             run(norm_variance, s - 6)
+            run(gelu_second, s - 1)
+            run(sort_words, s - 2)
+            for g in range(1, PASSES + 1):
+                next_pass(PASSES * (s + 2) + g)
+            run(interleave, s - 3)
+            run(quantise_h, s - 3)
             if s >= 8:
                 fill(1)
             run(quantise_x, s + 2)
@@ -535,54 +538,53 @@ def tile_structuralequationmodels_e_kernel(
             run(layer1, s)
             run(rows_of_h, s - 1)
             run(words_of_h, s - 2)
-            run(layer2, s - 4)
+            run(layer2, s - 3)
 
 
         last = D - 1
         norm_rstd(7)
-        gelu(13)
+        norm_mean(9)
+        gelu_half(13, 0)
+        norm_variance(8)
+        gelu_half(13, 1)
         sort_words(12)
         interleave(11)
-        norm_mean(8)
-        quantise_h(10)
-        norm_variance(8)
-        fill(2)
-        flush(0)
+        fill(3)
         quantise_h(11)
         layer1(14)
         rows_of_h(13)
         words_of_h(12)
-        layer2(10)
-        gelu(14)
+        layer2(11)
+        gelu_half(14, 0)
+        norm_variance(9)
+        gelu_half(14, 1)
         sort_words(13)
         interleave(12)
-        norm_mean(9)
-        fill(3)
+        norm_mean(10)
+        fill(4)
+        flush(0)
         quantise_h(12)
         layer1_half(last, 0)
         rows_of_h(14)
         words_of_h(13)
-        layer2(11)
+        layer2(12)
         gelu_half(last, 0)
         sort_words(14)
         interleave(13)
-        norm_mean(10)
-        fill(3)
-        norm_variance(9)
-        norm_variance(10)
-        quantise_h(13)
         norm_mean(11)
+        norm_variance(10)
         fill(3)
+        quantise_h(13)
         layer1_half(last, 1)
         words_of_h(14)
-        layer2(12)
         layer2(13)
+        norm_mean(12)
         gelu_half(last, 1)
         interleave(14)
         fill(2)
         rows_of_h(last, (0,), 0)
         rows_of_h(last, (1,), 4)
-        norm_mean(12)
+        norm_mean(13)
         fill(1)
         quantise_h(14)
         sort_words(last, (0,))
@@ -592,7 +594,7 @@ def tile_structuralequationmodels_e_kernel(
         layer2(14)
         norm_variance(11)
         norm_rstd(11)
-        norm_mean(13)
+        fill(1)
         interleave(last, (0,))
         interleave(last, (1,), nc.vector.tensor_copy)
         quantise_h(last, (0,))
@@ -600,20 +602,17 @@ def tile_structuralequationmodels_e_kernel(
         layer2(last, (0,), 0)
         layer2(last, (1,), 4)
         norm_variance(12)
-        norm_variance(13)
         norm_mean(14)
-        fill(2)
+        norm_variance(13)
+        fill(1)
         norm_mean(last, (0,))
         norm_mean(last, (1,))
-        norm_rstd_sqrt(13)
         norm_variance(14)
         norm_variance(last, (0,))
         norm_variance(last, (1,))
         norm_rstd_sqrt(last)
-        fill(2)
-        flush(0)
         fill(4)
-        norm_rstd_reciprocal(13)
-        fill(3)
+        flush(0)
+        fill(6)
         norm_rstd_reciprocal(last)
         fill(2 * D)

@@ -35,6 +35,11 @@ PAIR = 2
 FLOPS = 2 * B * D * (K * H + H * V)
 
 
+GROUPS = ((0, 4), (4, 4), (8, 6), (14, 2))
+LATE = (13, 15,)
+WIDE = 6
+
+
 def tile_structuralequationmodels_e_kernel(
     tc, causal_vars, adj_soft, W1_words, W1_scales, b1, W2_words, W2_scales, b2, gamma, beta, out
 ):
@@ -111,34 +116,40 @@ def tile_structuralequationmodels_e_kernel(
         def load_cv(g):
             nc.sync.dma_start(out=cv_rows[:, g, :, :], in_=cv_dram[:, :, K_PASS * g : K_PASS * (g + 1)])
 
-        def row_of(vector):
-            return vector.rearrange("i v -> (i v)").unsqueeze(0)
+        def load_row(tile, partition, vector):
+            row = vector.rearrange("i v -> (i v)").unsqueeze(0)
+            nc.gpsimd.dma_start(out=tile[partition : partition + 1, :], in_=row)
 
-        load_cv(0)
-        load_cv(1)
-        nc.vector.memset(adj_rows[:].bitcast(I32), 0)
-        nc.sync.dma_start(out=adj_rows[0:1, :], in_=row_of(adj_soft))
-        nc.vector.memset(b2_row[:].bitcast(I32), 0)
-        nc.scalar.dma_start(out=b2_row[0:1, :], in_=row_of(b2))
-        nc.vector.memset(b1_rows[:].bitcast(I32), 0)
-        nc.scalar.dma_start(out=b1_rows[0 : D * H_TILES, :], in_=b1.rearrange("i (c m) -> (i c) m", m=P))
-        load_cv(2)
-        load_cv(3)
+        def load_first_words(half):
+            cols = slice(H // 2 * half, H // 2 * (half + 1))
+            nc.sync.dma_start(out=live["w1_words", 0][:, :, cols], in_=w1_words_dram[:, 0:PASSES, cols])
+
+        for g in range(PASSES):
+            load_cv(g)
         nc.vector.memset(minus_half[:], -0.5)
         warm = keep.tile([P, 1], F32)
         nc.scalar.activation(out=warm[:], in_=minus_half[:, 0:1], func=ACT.Gelu)
+        nc.vector.memset(adj_rows[:].bitcast(I32), 0)
+        nc.sync.dma_start(out=adj_rows[0:1, :], in_=adj_soft.rearrange("i v -> (i v)").unsqueeze(0))
+        live["w1_words", 0] = work.tile([P, PASSES, H], I32, name="w1_words", bufs=W1_BUFS, align_bytes=64)
+        load_first_words(0)
+        nc.vector.memset(w1_planes[:, 0, :].bitcast(I32), 0)
+        load_w1_planes(0)
+        load_first_words(1)
         make_identity(nc, ident_f32[:])
+        nc.vector.memset(b2_row[:].bitcast(I32), 0)
+        load_row(b2_row, 0, b2)
         make_identity(nc, ident_bf16[:])
-        nc.vector.memset(w1_planes[:, 0:LOOKAHEAD, :].bitcast(I32), 0)
         nc.vector.memset(ones[:], 1.0)
-        nc.vector.memset(gain_rows[:].bitcast(I32), 0)
-        nc.gpsimd.dma_start(out=gain_rows[0:1, :], in_=row_of(gamma))
-        nc.gpsimd.dma_start(out=gain_rows[QUADRANT : QUADRANT + 1, :], in_=row_of(beta))
-        load_equation(0)
+        nc.vector.memset(b1_rows[:].bitcast(I32), 0)
+        nc.gpsimd.dma_start(out=b1_rows[0 : D * H_TILES, :], in_=b1.rearrange("i (c m) -> (i c) m", m=P))
+        nc.vector.memset(w1_planes[:, 1:LOOKAHEAD, :].bitcast(I32), 0)
         load_equation(1)
         load_equation(2)
         load_equation(3)
-
+        nc.vector.memset(gain_rows[:].bitcast(I32), 0)
+        load_row(gain_rows, 0, gamma)
+        load_row(gain_rows, QUADRANT, beta)
         nc.vector.memset(select[:].bitcast(I32), 0)
         for r in range(2):
             nc.vector.memset(select[QUADRANT * r : QUADRANT * r + 1, r, :], 1.0)
@@ -340,14 +351,21 @@ def tile_structuralequationmodels_e_kernel(
                 one_small_step()
 
         def group_of(i):
-            return (i - i % GROUP, GROUP)
+            for first, size in GROUPS:
+                if first <= i < first + size:
+                    return first, size
 
         def norm_variance(i, bts=(0, 1)):
             first, size = group_of(i)
             if i == first and bts[0] == 0:
-                live["square_sum", first] = work.tile([P, GROUP * B_TILES], F32, name="square_sum", bufs=4)
+                live["square_sum", first] = work.tile([P, WIDE * B_TILES], F32, name="square_sum", bufs=4)
             square_sum = live["square_sum", first]
             y_sum = live["y_sum", i - i % PAIR]
+            if i % PAIR == PAIR - 1 and bts[-1] == B_TILES - 1:
+                minus_mean = work.tile([P, PAIR * B_TILES], F32, name="minus_mean", bufs=8)
+                nc.scalar.mul(out=minus_mean[:], in_=y_sum[:], mul=-1.0 / V)
+                live["minus_mean", i - 1] = minus_mean[:, 0:B_TILES]
+                live["minus_mean", i] = minus_mean[:, B_TILES:]
             for bt in bts:
                 squares = work.tile([P, V], BF16, name="squares", bufs=4)
                 col = B_TILES * (i - first) + bt
@@ -360,14 +378,9 @@ def tile_structuralequationmodels_e_kernel(
                     scale=-float(V),
                     accum_out=square_sum[:, col : col + 1],
                 )
-            if i % PAIR == PAIR - 1 and bts[-1] == B_TILES - 1:
-                minus_mean = work.tile([P, PAIR * B_TILES], F32, name="minus_mean", bufs=8)
-                nc.scalar.mul(out=minus_mean[:], in_=y_sum[:], mul=-1.0 / V)
-                live["minus_mean", i - 1] = minus_mean[:, 0:B_TILES]
-                live["minus_mean", i] = minus_mean[:, B_TILES:]
-            if i == first + size - 1 and i < D - GROUP:
+            if i == first + size - 1 and i not in LATE:
                 n = B_TILES * size
-                var_eps = work.tile([P, GROUP * B_TILES], F32, name="var_eps", bufs=4)
+                var_eps = work.tile([P, WIDE * B_TILES], F32, name="var_eps", bufs=4)
                 nc.scalar.activation(
                     out=var_eps[:, 0:n],
                     in_=square_sum[:, 0:n],
@@ -380,7 +393,7 @@ def tile_structuralequationmodels_e_kernel(
         def norm_rstd_sqrt(i):
             first, size = group_of(i)
             n = B_TILES * size
-            std = work.tile([P, GROUP * B_TILES], F32, name="std")
+            std = work.tile([P, WIDE * B_TILES], F32, name="std")
             nc.scalar.activation(
                 out=std[:, 0:n], in_=live["square_sum", first][:, 0:n], func=ACT.Sqrt, bias=eps_col[:], scale=1.0 / V**3
             )
@@ -390,7 +403,7 @@ def tile_structuralequationmodels_e_kernel(
             first, size = group_of(i)
             n = B_TILES * size
             std = live["std", first]
-            rstd = work.tile([P, GROUP * B_TILES], F32, name="rstd")
+            rstd = work.tile([P, WIDE * B_TILES], F32, name="rstd")
             nc.vector.reciprocal(out=rstd[:, 0:n], in_=std[:, 0:n])
             live["rstd", first] = rstd[:, 0:n]
 
@@ -398,19 +411,20 @@ def tile_structuralequationmodels_e_kernel(
             first, size = group_of(i)
             if i != first + size - 1:
                 return
-            a = live["var_eps", first]
-            bits = work.tile([P, GROUP * B_TILES], I32, name="bits")
+            n = B_TILES * size
+            a = live["var_eps", first][:, 0:n]
+            bits = work.tile([P, n], I32, name="bits")
             small_steps.append(
                 lambda: nc.vector.tensor_scalar(
-                    out=bits[:], in0=a[:].bitcast(I32), scalar1=-0.5, scalar2=SEED, op0=ALU.mult, op1=ALU.add
+                    out=bits[:], in0=a.bitcast(I32), scalar1=-0.5, scalar2=SEED, op0=ALU.mult, op1=ALU.add
                 )
             )
             r = bits[:].bitcast(F32)
             for k in range(3):
-                square = work.tile([P, GROUP * B_TILES], F32, name="square%d" % k)
-                slope = work.tile([P, GROUP * B_TILES], F32, name="slope%d" % k)
-                better = work.tile([P, GROUP * B_TILES], F32, name="better%d" % k)
-                small_steps.extend(newton_step(a[:], r, square[:], slope[:], better[:]))
+                square = work.tile([P, n], F32, name="square%d" % k)
+                slope = work.tile([P, n], F32, name="slope%d" % k)
+                better = work.tile([P, n], F32, name="better%d" % k)
+                small_steps.extend(newton_step(a, r, square[:], slope[:], better[:]))
                 r = better[:]
             live["rstd", first] = r
 
@@ -438,26 +452,38 @@ def tile_structuralequationmodels_e_kernel(
                 one_small_step()
             live["centred", i] = centred
 
-        def norm_shift_and_store(i):
-            centred = live["centred", i]
+        def norm_shift(i, bt):
             first = i - i % PAIR
             group_first = group_of(i)[0]
-            rstd = live["rstd", group_first]
+            col = B_TILES * (i - group_first) + bt
+            nc.vector.scalar_tensor_tensor(
+                out=live["result", first][:, bt, i - first, :],
+                in0=live["centred", i][:, bt, :],
+                scalar=live["rstd", group_first][:, col : col + 1],
+                in1=beta_rows[:, V * i : V * (i + 1)],
+                op0=ALU.mult,
+                op1=ALU.add,
+            )
+            one_small_step()
+
+        def norm_shift_and_store(i):
+            first = i - i % PAIR
             if i == first:
                 live["result", first] = work.tile([P, B_TILES, PAIR, V], F32, name="result", bufs=8)
-            result = live["result", first]
             for bt in range(B_TILES):
-                nc.vector.scalar_tensor_tensor(
-                    out=result[:, bt, i - first, :],
-                    in0=centred[:, bt, :],
-                    scalar=rstd[:, B_TILES * (i - group_first) + bt : B_TILES * (i - group_first) + bt + 1],
-                    in1=beta_rows[:, V * i : V * (i + 1)],
-                    op0=ALU.mult,
-                    op1=ALU.add,
-                )
-                one_small_step()
+                norm_shift(i, bt)
             if i == first + PAIR - 1:
-                nc.sync.dma_start(out=out_dram[:, :, first : first + PAIR, :], in_=result[:])
+                nc.sync.dma_start(out=out_dram[:, :, first : first + PAIR, :], in_=live["result", first][:])
+
+        def shift_and_store_last_pair():
+            first = D - PAIR
+            live["result", first] = work.tile([P, B_TILES, PAIR, V], F32, name="result", bufs=8)
+            for bt in range(B_TILES):
+                for i in (first, first + 1):
+                    norm_shift(i, bt)
+                nc.sync.dma_start(
+                    out=out_dram[:, bt, first : first + PAIR, :], in_=live["result", first][:, bt, :, :]
+                )
 
         def run(stage, i):
             if 0 <= i < D:
@@ -505,6 +531,8 @@ def tile_structuralequationmodels_e_kernel(
         LAG = 4
         rest = []
         rest_of_norm()
+        rest.remove((norm_shift_and_store, D - 2))
+        rest.remove((norm_shift_and_store, D - 1))
 
         def ready(stage, j):
             if stage is norm_gain:
@@ -549,7 +577,7 @@ def tile_structuralequationmodels_e_kernel(
         gelu_half(13, 1)
         sort_words(12)
         interleave(11)
-        fill(3)
+        fill(4)
         quantise_h(11)
         layer1(14)
         rows_of_h(13)
@@ -593,7 +621,6 @@ def tile_structuralequationmodels_e_kernel(
         words_of_h(last, (1,), 5)
         layer2(14)
         norm_variance(11)
-        norm_rstd(11)
         fill(1)
         interleave(last, (0,))
         interleave(last, (1,), nc.vector.tensor_copy)
@@ -604,15 +631,17 @@ def tile_structuralequationmodels_e_kernel(
         norm_variance(12)
         norm_mean(14)
         norm_variance(13)
-        fill(1)
+        norm_rstd_sqrt(13)
+        fill(2)
         norm_mean(last, (0,))
         norm_mean(last, (1,))
         norm_variance(14)
         norm_variance(last, (0,))
         norm_variance(last, (1,))
         norm_rstd_sqrt(last)
-        fill(4)
-        flush(0)
-        fill(6)
+        fill(1)
+        norm_rstd_reciprocal(13)
+        fill(10)
         norm_rstd_reciprocal(last)
         fill(2 * D)
+        shift_and_store_last_pair()

from contextlib import ExitStack

import concourse.mybir as mybir
from concourse.masks import make_identity

F32 = mybir.dt.float32
BF16 = mybir.dt.bfloat16
I32 = mybir.dt.int32
U32 = mybir.dt.uint32
U8 = mybir.dt.uint8
FP8X4 = mybir.dt.float8_e4m3fn_x4
ALU = mybir.AluOpType
ACT = mybir.ActivationFunctionType

P = 128
PACK = 4
K_PASS = P * PACK
B, D, V, H = 256, 16, 128, 512
K = D * V
PASSES = K // K_PASS
B_TILES = B // P
H_TILES = H // P
QUADRANT = 32
QUADRANTS = P // QUADRANT
LIVE = 4
BANK = 512
LN_EPS = 1e-5
W2_GROUP = 4
LOOKAHEAD = 4
W1_BUFS = 10
GROUP = 4
SEED = 1597463007.0
PAIR = 2

FLOPS = 2 * B * D * (K * H + H * V)


GROUPS = ((0, 4), (4, 4), (8, 6), (14, 2))
LATE = (13, 15,)
WIDE = 6


def tile_structuralequationmodels_e_kernel(
    tc, causal_vars, adj_soft, W1_words, W1_scales, b1, W2_words, W2_scales, b2, gamma, beta, out
):
    nc = tc.nc

    w1_words_dram = W1_words.rearrange("g p n t -> g p (n t)").bitcast(I32).rearrange("g p n -> p g n")
    w1_scales_dram = W1_scales.bitcast(I32).rearrange("(i g) q n -> i g q n", g=PASSES)
    w2_words_dram = W2_words.rearrange("i p v t -> i p (v t)").bitcast(I32).rearrange("i p v -> p i v")
    w2_scales_dram = W2_scales.bitcast(I32).rearrange("i q v -> q i v")
    cv_dram = causal_vars.rearrange("(c b) j v -> b c (j v)", b=P)
    out_dram = out.rearrange("(c b) i v -> b c i v", b=P)

    with ExitStack() as ctx:
        ctx.enter_context(tc.manual_schedule())
        keep = ctx.enter_context(tc.tile_pool(name="keep", bufs=1))
        work = ctx.enter_context(tc.tile_pool(name="work", bufs=2))
        psum = ctx.enter_context(tc.psum_pool(name="psum", bufs=1))

        live = {}

        def bank(k, shape, dtype, name):
            return psum.tile(shape, dtype, name=name, tag="bank%d" % k)

        ident_f32 = keep.tile([P, P], F32)
        ident_bf16 = keep.tile([P, P], BF16)
        adj_col = keep.tile([P, D, PASSES], F32)
        b1_col = keep.tile([P, D * H_TILES], F32)
        minus_half = keep.tile([P, PAIR * B_TILES], F32)
        eps_col = keep.tile([P, 1], F32)
        cv_mx = keep.tile([P, PASSES * B * PACK], BF16, align_bytes=64)
        w1_planes = keep.tile([P, D, H], U8, align_bytes=64)
        w2_words = keep.tile([P, D, V], I32, align_bytes=64)
        w2_planes = keep.tile([P, D, V], U8, align_bytes=64)
        b2_rows = keep.tile([P, D * V], BF16)
        gamma_rows = keep.tile([P, D * V], BF16)
        beta_rows = keep.tile([P, D * V], BF16)
        cv_rows = work.tile([P, PASSES, B_TILES, K_PASS], BF16, name="cv_rows", tag="x", bufs=3, align_bytes=64)
        b2_row = keep.tile([P, D * V], BF16)
        gain_rows = keep.tile([P, D * V], BF16)
        select = keep.tile([P, 2, P], BF16)
        ones = keep.tile([P, P], BF16)
        adj_rows = keep.tile([P, D * D], BF16)
        b1_rows = keep.tile([P, P], BF16)

        def load_w1_planes(i):
            for quadrant in range(QUADRANTS):
                first = QUADRANT * quadrant
                nc.sync.dma_start(
                    out=w1_planes[first : first + PASSES * LIVE, i, :].bitcast(I32),
                    in_=w1_scales_dram[i, :, LIVE * quadrant : LIVE * (quadrant + 1), :],
                )

        def load_w2_planes():
            for r in range(LIVE):
                nc.sync.dma_start(
                    out=w2_planes[r:P:QUADRANT, :, :].bitcast(I32), in_=w2_scales_dram[r : QUADRANTS * LIVE : LIVE, :, :]
                )

        def load_w2_words(i):
            if i % W2_GROUP == 0:
                nc.sync.dma_start(out=w2_words[:, i : i + W2_GROUP, :], in_=w2_words_dram[:, i : i + W2_GROUP, :])

        def load_equation(i):
            load_w1_planes(i)
            w1_words = work.tile([P, PASSES, H], I32, name="w1_words", bufs=W1_BUFS, align_bytes=64)
            if i == 0:
                for half in range(2):
                    cols = slice(H // 2 * half, H // 2 * (half + 1))
                    nc.sync.dma_start(out=w1_words[:, :, cols], in_=w1_words_dram[:, 0:PASSES, cols])
            else:
                nc.sync.dma_start(out=w1_words[:], in_=w1_words_dram[:, PASSES * i : PASSES * (i + 1), :])
            live["w1_words", i] = w1_words

        def load_cv(g):
            nc.sync.dma_start(out=cv_rows[:, g, :, :], in_=cv_dram[:, :, K_PASS * g : K_PASS * (g + 1)])

        def load_row(tile, partition, vector):
            row = vector.rearrange("i v -> (i v)").unsqueeze(0)
            nc.gpsimd.dma_start(out=tile[partition : partition + 1, :], in_=row)

        def load_first_words(half):
            cols = slice(H // 2 * half, H // 2 * (half + 1))
            nc.sync.dma_start(out=live["w1_words", 0][:, :, cols], in_=w1_words_dram[:, 0:PASSES, cols])

        for g in range(PASSES):
            load_cv(g)
        nc.vector.memset(minus_half[:], -0.5)
        warm = keep.tile([P, 1], F32)
        nc.scalar.activation(out=warm[:], in_=minus_half[:, 0:1], func=ACT.Gelu)
        nc.vector.memset(adj_rows[:].bitcast(I32), 0)
        nc.sync.dma_start(out=adj_rows[0:1, :], in_=adj_soft.rearrange("i v -> (i v)").unsqueeze(0))
        live["w1_words", 0] = work.tile([P, PASSES, H], I32, name="w1_words", bufs=W1_BUFS, align_bytes=64)
        load_first_words(0)
        nc.vector.memset(w1_planes[:, 0, :].bitcast(I32), 0)
        load_w1_planes(0)
        load_first_words(1)
        make_identity(nc, ident_f32[:])
        nc.vector.memset(b2_row[:].bitcast(I32), 0)
        load_row(b2_row, 0, b2)
        make_identity(nc, ident_bf16[:])
        nc.vector.memset(ones[:], 1.0)
        nc.vector.memset(b1_rows[:].bitcast(I32), 0)
        nc.gpsimd.dma_start(out=b1_rows[0 : D * H_TILES, :], in_=b1.rearrange("i (c m) -> (i c) m", m=P))
        nc.vector.memset(w1_planes[:, 1:LOOKAHEAD, :].bitcast(I32), 0)
        load_equation(1)
        load_equation(2)
        load_equation(3)
        nc.vector.memset(gain_rows[:].bitcast(I32), 0)
        load_row(gain_rows, 0, gamma)
        load_row(gain_rows, QUADRANT, beta)
        nc.vector.memset(select[:].bitcast(I32), 0)
        for r in range(2):
            nc.vector.memset(select[QUADRANT * r : QUADRANT * r + 1, r, :], 1.0)
        nc.vector.tensor_scalar(
            out=eps_col[:], in0=minus_half[:, 0:1], scalar1=0.0, scalar2=LN_EPS, op0=ALU.mult, op1=ALU.add
        )

        def repeat_row(rows, pick, repeated):
            for j in range(D * V // (2 * BANK)):
                row_psum = bank(6 + j, [P, 2 * BANK], BF16, "row_psum")
                for half in range(2):
                    nc.tensor.matmul(
                        row_psum[:, BANK * half : BANK * (half + 1)],
                        lhsT=pick,
                        rhs=rows[:, 2 * BANK * j + BANK * half : 2 * BANK * j + BANK * (half + 1)],
                        start=True,
                        stop=True,
                    )
                nc.scalar.copy(out=repeated[:, 2 * BANK * j : 2 * BANK * (j + 1)], in_=row_psum[:])

        def transpose_cv(g):
            cv_psum = bank(g, [P, 2, B_TILES, P], F32, "cv_psum")
            for c in range(B_TILES):
                words = cv_rows[:, g, c, :].bitcast(F32)
                for u in range(2):
                    nc.tensor.transpose(cv_psum[:, u, c, :], words[:, u : 2 * P : 2], ident_f32[:])
            nc.scalar.copy(
                out=cv_mx[:, B * PACK * g : B * PACK * (g + 1)].bitcast(F32).rearrange("p (b u) -> p b u", u=2),
                in_=cv_psum[:].rearrange("p u c b -> p (c b) u"),
            )

        transpose_cv(0)
        adj_psum = bank(4, [P, D * D], F32, "adj_psum")
        nc.tensor.matmul(adj_psum[:], lhsT=ones[:], rhs=adj_rows[:], start=True, stop=True)
        adj_by_quadrant = adj_psum[:].rearrange("p (i g q) -> p i g q", g=PASSES, q=QUADRANTS)
        for quadrant in range(QUADRANTS):
            rows = slice(QUADRANT * quadrant, QUADRANT * (quadrant + 1))
            nc.vector.tensor_copy(out=adj_col[rows, :, :], in_=adj_by_quadrant[rows, :, :, quadrant])
        for g in range(1, PASSES):
            transpose_cv(g)
        repeat_row(b2_row, ones[:], b2_rows)
        b1_psum = bank(5, [P, P], BF16, "b1_psum")
        nc.tensor.transpose(b1_psum[:], b1_rows[:], ident_bf16[:])
        nc.scalar.copy(out=b1_col[:], in_=b1_psum[:, 0 : D * H_TILES])

        small_steps = []

        def one_small_step():
            if small_steps:
                small_steps.pop(0)()

        def scale_pass(i, g):
            if g == 0:
                live["x", i] = work.tile([P, PASSES * B * PACK], BF16, name="x", tag="x", bufs=3, align_bytes=64)
            cols = slice(B * PACK * g, B * PACK * (g + 1))
            nc.vector.tensor_scalar_mul(
                out=live["x", i][:, cols], in0=cv_mx[:, cols], scalar1=adj_col[:, i, g : g + 1]
            )
            one_small_step()

        def next_pass(k):
            if k < D * PASSES:
                scale_pass(k // PASSES, k % PASSES)

        def quantise_passes(i, first, last):
            if first == 0:
                live["x_codes", i] = work.tile([P, PASSES * B], U32, name="x_codes", bufs=3, align_bytes=64)
                live["x_plane", i] = work.tile([P, PASSES * B], U8, name="x_plane", bufs=3, align_bytes=64)
            nc.vector.quantize_mx(
                out=live["x_codes", i][:, B * first : B * last].bitcast(FP8X4),
                scales=live["x_plane", i][:, B * first : B * last],
                in_=live["x", i][:, B * PACK * first : B * PACK * last],
            )
            one_small_step()

        def quantise_x(i):
            quantise_passes(i, 0, PASSES)

        def layer1_half(i, half):
            x_codes = live["x_codes", i]
            x_plane = live["x_plane", i]
            h_psum = bank(2 * (i % 2) + half, [P, 2, B], F32, "h_psum")
            for c2 in range(2):
                n_cols = slice(P * (2 * half + c2), P * (2 * half + c2 + 1))
                for g in range(PASSES):
                    b_cols = slice(B * g, B * (g + 1))
                    nc.tensor.matmul_mx(
                        out=h_psum[:, c2, :],
                        lhsT=live["w1_words", i][:, g, n_cols].bitcast(FP8X4),
                        lhsT_scale=w1_planes[LIVE * g :, i, n_cols],
                        rhs=x_codes[:, b_cols].bitcast(FP8X4),
                        rhs_scale=x_plane[:, b_cols],
                        start=(g == 0),
                        stop=(g == PASSES - 1),
                    )
            live["h_psum", i, half] = h_psum

        def layer1(i):
            layer1_half(i, 0)
            layer1_half(i, 1)

        def gelu_half(i, half):
            if half == 0:
                live["h_cols", i] = work.tile([P, H_TILES, B], BF16, name="h_cols")
            for c in (2 * half, 2 * half + 1):
                nc.scalar.activation(
                    out=live["h_cols", i][:, c, :],
                    in_=live["h_psum", i, half][:, c % 2, :],
                    func=ACT.Gelu,
                    bias=b1_col[:, H_TILES * i + c : H_TILES * i + c + 1],
                    scale=1.0,
                )

        def gelu(i):
            gelu_half(i, 0)
            gelu_half(i, 1)

        def rows_of_h(i, bts=(0, 1), k=4):
            h_rows_psum = bank(k, [P, B_TILES, H], BF16, "h_rows_psum")
            for bt in bts:
                live["h_rows_psum", i, bt] = h_rows_psum
                for c in range(H_TILES):
                    nc.tensor.matmul(
                        h_rows_psum[:, bt, P * c : P * (c + 1)],
                        lhsT=live["h_cols", i][:, c, P * bt : P * (bt + 1)],
                        rhs=ident_bf16[:],
                        start=True,
                        stop=True,
                    )

        def sort_words(i, bts=(0, 1), copy=nc.scalar.copy):
            if bts[0] == 0:
                live["h_rows", i] = work.tile([P, B_TILES, 2, P], F32, name="h_rows")
            tiles = slice(bts[0], bts[-1] + 1)
            copy(
                out=live["h_rows", i][:, tiles, :, :],
                in_=live["h_rows_psum", i, bts[0]][:, tiles, :].bitcast(F32).rearrange("b c (p u) -> b c u p", u=2),
            )

        def words_of_h(i, bts=(0, 1), k=5):
            h_words_psum = bank(k, [P, 2, B_TILES, P], F32, "h_words_psum")
            for bt in bts:
                live["h_words_psum", i, bt] = h_words_psum
                for u in range(2):
                    nc.tensor.transpose(h_words_psum[:, u, bt, :], live["h_rows", i][:, bt, u, :], ident_f32[:])

        def interleave(i, bts=(0, 1), copy=nc.scalar.copy):
            if bts[0] == 0:
                live["h_mx", i] = work.tile([P, B * PACK], BF16, name="h_mx", align_bytes=64)
            tiles = slice(bts[0], bts[-1] + 1)
            cols = slice(P * PACK * bts[0], P * PACK * (bts[-1] + 1))
            copy(
                out=live["h_mx", i][:, cols].bitcast(F32).rearrange("p (b u) -> p b u", u=2),
                in_=live["h_words_psum", i, bts[0]][:, :, tiles, :].rearrange("p u c b -> p (c b) u"),
            )

        def quantise_h(i, bts=(0, 1)):
            if bts[0] == 0:
                live["h_codes", i] = work.tile([P, B], U32, name="h_codes", bufs=3, align_bytes=64)
                live["h_plane", i] = work.tile([P, B], U8, name="h_plane", bufs=3, align_bytes=64)
            cols = slice(P * bts[0], P * (bts[-1] + 1))
            nc.vector.quantize_mx(
                out=live["h_codes", i][:, cols].bitcast(FP8X4),
                scales=live["h_plane", i][:, cols],
                in_=live["h_mx", i][:, PACK * P * bts[0] : PACK * P * (bts[-1] + 1)],
            )
            one_small_step()

        def layer2(i, bts=(0, 1), k=None):
            y_psum = bank(6 + i % 2 if k is None else k, [P, B_TILES, V], F32, "y_psum")
            for bt in bts:
                live["y_psum", i, bt] = y_psum
                b_cols = slice(P * bt, P * (bt + 1))
                nc.tensor.matmul_mx(
                    out=y_psum[:, bt, :],
                    lhsT=live["h_codes", i][:, b_cols].bitcast(FP8X4),
                    lhsT_scale=live["h_plane", i][:, b_cols],
                    rhs=w2_words[:, i, :].bitcast(FP8X4),
                    rhs_scale=w2_planes[:, i, :],
                    start=True,
                    stop=True,
                )

        def norm_mean(i, bts=(0, 1)):
            if bts[0] == 0:
                live["y", i] = work.tile([P, B_TILES, V], F32, name="y", bufs=13)
                if i % PAIR == 0:
                    live["y_sum", i] = work.tile([P, PAIR * B_TILES], F32, name="y_sum", bufs=8)
            for bt in bts:
                nc.vector.scalar_tensor_tensor(
                    out=live["y", i][:, bt, :],
                    in0=live["y_psum", i, bt][:, bt, :],
                    scalar=1.0,
                    in1=b2_rows[:, V * i : V * (i + 1)],
                    op0=ALU.mult,
                    op1=ALU.add,
                    accum_out=live["y_sum", i - i % PAIR][:, B_TILES * (i % PAIR) + bt : B_TILES * (i % PAIR) + bt + 1],
                )
                one_small_step()

        def group_of(i):
            for first, size in GROUPS:
                if first <= i < first + size:
                    return first, size

        def norm_variance(i, bts=(0, 1)):
            first, size = group_of(i)
            if i == first and bts[0] == 0:
                live["square_sum", first] = work.tile([P, WIDE * B_TILES], F32, name="square_sum", bufs=4)
            square_sum = live["square_sum", first]
            y_sum = live["y_sum", i - i % PAIR]
            if i % PAIR == PAIR - 1 and bts[-1] == B_TILES - 1:
                minus_mean = work.tile([P, PAIR * B_TILES], F32, name="minus_mean", bufs=8)
                nc.scalar.mul(out=minus_mean[:], in_=y_sum[:], mul=-1.0 / V)
                live["minus_mean", i - 1] = minus_mean[:, 0:B_TILES]
                live["minus_mean", i] = minus_mean[:, B_TILES:]
            for bt in bts:
                squares = work.tile([P, V], BF16, name="squares", bufs=4)
                col = B_TILES * (i - first) + bt
                pair_col = B_TILES * (i % PAIR) + bt
                nc.scalar.activation(
                    out=squares[:],
                    in_=live["y", i][:, bt, :],
                    func=ACT.Square,
                    bias=y_sum[:, pair_col : pair_col + 1],
                    scale=-float(V),
                    accum_out=square_sum[:, col : col + 1],
                )
            if i == first + size - 1 and i not in LATE:
                n = B_TILES * size
                var_eps = work.tile([P, WIDE * B_TILES], F32, name="var_eps", bufs=4)
                nc.scalar.activation(
                    out=var_eps[:, 0:n],
                    in_=square_sum[:, 0:n],
                    func=ACT.Identity,
                    bias=eps_col[:],
                    scale=1.0 / V**3,
                )
                live["var_eps", first] = var_eps

        def norm_rstd_sqrt(i):
            first, size = group_of(i)
            n = B_TILES * size
            std = work.tile([P, WIDE * B_TILES], F32, name="std")
            nc.scalar.activation(
                out=std[:, 0:n], in_=live["square_sum", first][:, 0:n], func=ACT.Sqrt, bias=eps_col[:], scale=1.0 / V**3
            )
            live["std", first] = std

        def norm_rstd_reciprocal(i):
            first, size = group_of(i)
            n = B_TILES * size
            std = live["std", first]
            rstd = work.tile([P, WIDE * B_TILES], F32, name="rstd")
            nc.vector.reciprocal(out=rstd[:, 0:n], in_=std[:, 0:n])
            live["rstd", first] = rstd[:, 0:n]

        def norm_rstd(i):
            first, size = group_of(i)
            if i != first + size - 1:
                return
            n = B_TILES * size
            a = live["var_eps", first][:, 0:n]
            bits = work.tile([P, n], I32, name="bits")
            small_steps.append(
                lambda: nc.vector.tensor_scalar(
                    out=bits[:], in0=a.bitcast(I32), scalar1=-0.5, scalar2=SEED, op0=ALU.mult, op1=ALU.add
                )
            )
            r = bits[:].bitcast(F32)
            for k in range(3):
                square = work.tile([P, n], F32, name="square%d" % k)
                slope = work.tile([P, n], F32, name="slope%d" % k)
                better = work.tile([P, n], F32, name="better%d" % k)
                small_steps.extend(newton_step(a, r, square[:], slope[:], better[:]))
                r = better[:]
            live["rstd", first] = r

        def newton_step(a, r, square, slope, better):
            stt = nc.vector.scalar_tensor_tensor
            return [
                lambda: nc.vector.tensor_tensor(out=square, in0=r, in1=r, op=ALU.mult),
                lambda: stt(out=slope, in0=square, scalar=-0.5, in1=a, op0=ALU.mult, op1=ALU.mult),
                lambda: stt(out=better, in0=slope, scalar=1.5, in1=r, op0=ALU.add, op1=ALU.mult),
            ]

        def norm_gain(i):
            y = live["y", i]
            minus_mean = live["minus_mean", i]
            centred = work.tile([P, B_TILES, V], F32, name="centred", bufs=9)
            for bt in range(B_TILES):
                nc.vector.scalar_tensor_tensor(
                    out=centred[:, bt, :],
                    in0=y[:, bt, :],
                    scalar=minus_mean[:, bt : bt + 1],
                    in1=gamma_rows[:, V * i : V * (i + 1)],
                    op0=ALU.add,
                    op1=ALU.mult,
                )
                one_small_step()
            live["centred", i] = centred

        def norm_shift(i, bt):
            first = i - i % PAIR
            group_first = group_of(i)[0]
            col = B_TILES * (i - group_first) + bt
            nc.vector.scalar_tensor_tensor(
                out=live["result", first][:, bt, i - first, :],
                in0=live["centred", i][:, bt, :],
                scalar=live["rstd", group_first][:, col : col + 1],
                in1=beta_rows[:, V * i : V * (i + 1)],
                op0=ALU.mult,
                op1=ALU.add,
            )
            one_small_step()

        def norm_shift_and_store(i):
            first = i - i % PAIR
            if i == first:
                live["result", first] = work.tile([P, B_TILES, PAIR, V], F32, name="result", bufs=8)
            for bt in range(B_TILES):
                norm_shift(i, bt)
            if i == first + PAIR - 1:
                nc.sync.dma_start(out=out_dram[:, :, first : first + PAIR, :], in_=live["result", first][:])

        def shift_and_store_last_pair():
            first = D - PAIR
            live["result", first] = work.tile([P, B_TILES, PAIR, V], F32, name="result", bufs=8)
            for bt in range(B_TILES):
                for i in (first, first + 1):
                    norm_shift(i, bt)
                nc.sync.dma_start(
                    out=out_dram[:, bt, first : first + PAIR, :], in_=live["result", first][:, bt, :, :]
                )

        def run(stage, i):
            if 0 <= i < D:
                stage(i)

        def layer1_first(i):
            layer1_half(i, 0)

        def layer1_second(i):
            layer1_half(i, 1)

        def gelu_first(i):
            gelu_half(i, 0)

        def gelu_second(i):
            gelu_half(i, 1)

        def flush(i):
            while small_steps:
                one_small_step()

        scale_pass(0, 0)
        for g in range(1, PASSES):
            scale_pass(0, g)
            quantise_passes(0, g - 1, g)
        quantise_passes(0, PASSES - 1, PASSES)
        next_pass(PASSES)
        for g in range(1, PASSES + 1):
            next_pass(PASSES + g)
        quantise_x(1)
        nc.vector.memset(w2_planes[:].bitcast(I32), 0)
        load_w2_planes()
        load_w2_words(0)
        nc.vector.memset(w1_planes[:, LOOKAHEAD:, :].bitcast(I32), 0)

        repeats = {1: (gain_rows, select[:, 0, :], gamma_rows), 2: (gain_rows, select[:, 1, :], beta_rows)}

        def rest_of_norm():
            for j in range(D + LAG):
                if j < D:
                    rest.append((norm_gain, j))
                if j >= LAG:
                    rest.append((norm_shift_and_store, j - LAG))

        LAG = 4
        rest = []
        rest_of_norm()
        rest.remove((norm_shift_and_store, D - 2))
        rest.remove((norm_shift_and_store, D - 1))

        def ready(stage, j):
            if stage is norm_gain:
                return ("minus_mean", j) in live
            return ("rstd", group_of(j)[0]) in live and not small_steps

        def fill(n):
            for stage, j in [item for item in rest if ready(*item)][:n]:
                rest.remove((stage, j))
                stage(j)

        for s in range(D - 2):
            run(load_equation, s + LOOKAHEAD)
            run(load_w2_words, s + LOOKAHEAD)
            run(norm_rstd, s - 7)
            run(norm_mean, s - 5)
            run(gelu_first, s - 1)
            run(norm_variance, s - 6)
            run(gelu_second, s - 1)
            run(sort_words, s - 2)
            for g in range(1, PASSES + 1):
                next_pass(PASSES * (s + 2) + g)
            run(interleave, s - 3)
            run(quantise_h, s - 3)
            if s >= 8:
                fill(1)
            run(quantise_x, s + 2)
            flush(0)
            if s in repeats:
                repeat_row(*repeats[s])
            run(layer1, s)
            run(rows_of_h, s - 1)
            run(words_of_h, s - 2)
            run(layer2, s - 3)


        last = D - 1
        norm_rstd(7)
        norm_mean(9)
        gelu_half(13, 0)
        norm_variance(8)
        gelu_half(13, 1)
        sort_words(12)
        interleave(11)
        fill(4)
        quantise_h(11)
        layer1(14)
        rows_of_h(13)
        words_of_h(12)
        layer2(11)
        gelu_half(14, 0)
        norm_variance(9)
        gelu_half(14, 1)
        sort_words(13)
        interleave(12)
        norm_mean(10)
        fill(4)
        flush(0)
        quantise_h(12)
        layer1_half(last, 0)
        rows_of_h(14)
        words_of_h(13)
        layer2(12)
        gelu_half(last, 0)
        sort_words(14)
        interleave(13)
        norm_mean(11)
        norm_variance(10)
        fill(3)
        quantise_h(13)
        layer1_half(last, 1)
        words_of_h(14)
        layer2(13)
        norm_mean(12)
        gelu_half(last, 1)
        interleave(14)
        fill(2)
        rows_of_h(last, (0,), 0)
        rows_of_h(last, (1,), 4)
        norm_mean(13)
        fill(1)
        quantise_h(14)
        sort_words(last, (0,))
        sort_words(last, (1,), nc.vector.tensor_copy)
        words_of_h(last, (0,), 1)
        words_of_h(last, (1,), 5)
        layer2(14)
        norm_variance(11)
        fill(1)
        interleave(last, (0,))
        interleave(last, (1,), nc.vector.tensor_copy)
        quantise_h(last, (0,))
        quantise_h(last, (1,))
        layer2(last, (0,), 0)
        layer2(last, (1,), 4)
        norm_variance(12)
        norm_mean(14)
        norm_variance(13)
        norm_rstd_sqrt(13)
        fill(2)
        norm_mean(last, (0,))
        norm_mean(last, (1,))
        norm_variance(14)
        norm_variance(last, (0,))
        norm_variance(last, (1,))
        norm_rstd_sqrt(last)
        fill(1)
        norm_rstd_reciprocal(13)
        fill(10)
        norm_rstd_reciprocal(last)
        fill(2 * D)
        shift_and_store_last_pair()
